import numpy as np
import ml_dtypes


def mxq(x, axis, fmt="e4m3"):
    dtype, down = {"e4m3": (ml_dtypes.float8_e4m3fn, 7), "e5m2": (ml_dtypes.float8_e5m2, 14)}[fmt]
    v = np.moveaxis(np.asarray(x, np.float32).astype(ml_dtypes.bfloat16).astype(np.float64), axis, -1)
    blocks = v.reshape(v.shape[:-1] + (-1, 32))
    amax = np.abs(blocks).max(-1, keepdims=True)
    byte = np.maximum(np.where(amax > 0, np.frexp(amax)[1] - 1 + 127, 0) - down, 1)
    scale = np.exp2(byte - 127.0)
    codes = (blocks / scale).astype(np.float32).astype(dtype).astype(np.float64)
    return np.moveaxis((codes * scale).reshape(v.shape), -1, axis)


WIDE = False


def mx_kscale(k):
    if not WIDE:
        return np.ones(k)
    levels = np.array([30, -30])
    if k % 512:
        return np.exp2(np.random.permutation(np.resize(levels, k // 32))).repeat(32)
    a = np.empty((k // 512, 16))
    for p in range(k // 512):
        a[p, :8] = np.random.permutation(np.resize(levels, 8))
        for g in range(8):
            far = levels[np.abs(levels - a[p, g]) >= 10]
            a[p, g + 8] = far[np.random.randint(len(far))]
    return np.exp2(a.ravel()).repeat(32)


BF16 = ml_dtypes.bfloat16


def bf(x):
    return np.asarray(x, np.float32).astype(BF16)


def f64(x):
    return np.asarray(x).astype(np.float64)


E2M1 = np.array([0.0, 0.5, 1.0, 1.5, 2.0, 3.0, 4.0, 6.0, -0.0, -0.5, -1.0, -1.5, -2.0, -3.0, -4.0, -6.0])


def pack_weight(w, fmt):
    k, n = w.shape
    w = f64(bf(w)).reshape(k // 32, 32, n)
    amax = np.abs(w).max(1)
    if fmt == "e4m3":
        byte = np.frexp(amax)[1] - 1 + 127 - 7
    else:
        mant, ex = np.frexp(amax / 6.0)
        byte = np.where(mant > 0.5, ex, ex - 1) + 127
    byte = np.clip(np.where(amax > 0, byte, 1), 1, 254)
    scaled = (w * np.exp2(127.0 - byte)[:, None, :]).reshape(k, n).astype(np.float32)
    by_word = np.ascontiguousarray(scaled.reshape(k // 512, 128, 4, n).transpose(0, 1, 3, 2))
    if fmt == "e4m3":
        words = by_word.astype(ml_dtypes.float8_e4m3fn).view(np.uint8)
    else:
        c = by_word.astype(ml_dtypes.float4_e2m1fn).view(np.uint8) & 0xF
        words = c[..., 0::2] | (c[..., 1::2] << 4)
    return np.ascontiguousarray(words), np.ascontiguousarray(byte.astype(np.uint8).reshape(k // 512, 16, n))


def unpack_weight(words, scales, fmt):
    g, p, n, _ = words.shape
    if fmt == "e4m3":
        vals = np.ascontiguousarray(words).view(ml_dtypes.float8_e4m3fn).astype(np.float64)
    else:
        nib = np.empty((g, p, n, 4), np.uint8)
        nib[..., 0::2] = words & 0xF
        nib[..., 1::2] = words >> 4
        vals = E2M1[nib]
    vals = vals * np.repeat(np.exp2(scales.astype(np.float64) - 127.0), 8, axis=1)[..., None]
    return vals.transpose(0, 1, 3, 2).reshape(g * 512, n)

def pack4(w):
    words, scales = pack_weight(w, "e2m1")
    return words.reshape(words.shape[0], 128, -1), scales


def unpack4(words, scales):
    return unpack_weight(words.reshape(words.shape[0], 128, -1, 2), scales, "e2m1")


B, F, Hh, Ww, DIN, NH, HD = 1, 2, 16, 32, 1536, 12, 128
L = F * Hh * Ww
DIM = NH * HD
C = HD // 2
EPS = 1e-6


def rope_angles():
    tc = C - 2 * (C // 3)
    hc = C // 3
    wc = C // 3

    def ax(n, dh):
        inv = 1.0 / np.power(10000.0, np.arange(dh) * 2.0 / (2 * dh))
        return np.outer(np.arange(n), inv)

    ft, fh, fw = ax(F, tc), ax(Hh, hc), ax(Ww, wc)
    return np.concatenate([
        np.broadcast_to(ft[:, None, None, :], (F, Hh, Ww, tc)),
        np.broadcast_to(fh[None, :, None, :], (F, Hh, Ww, hc)),
        np.broadcast_to(fw[None, None, :, :], (F, Hh, Ww, wc)),
    ], axis=-1).reshape(L, C)


def rms(u, g):
    return u / np.sqrt(np.mean(u * u, axis=-1, keepdims=True) + EPS) * g


def rope(u, cos, sin):
    us = u.reshape(B, L, NH, C, 2)
    ur, ui = us[..., 0], us[..., 1]
    c = cos[None, :, None, :]
    s = sin[None, :, None, :]
    return np.stack([ur * c - ui * s, ur * s + ui * c], axis=-1).reshape(B, L, NH, HD)


def setup_inputs():
    s = mx_kscale(DIN)
    ang = rope_angles()
    x = bf(np.random.standard_normal((B, L, DIN)) * s)
    wq_words, wq_scales = pack4(np.random.standard_normal((DIN, DIM)) / np.sqrt(DIN) / s[:, None])
    wk_words, wk_scales = pack4(np.random.standard_normal((DIN, DIM)) / np.sqrt(DIN) / s[:, None])
    return {"x": x,
            "wq_words": wq_words,
            "wq_scales": wq_scales,
            "wk_words": wk_words,
            "wk_scales": wk_scales,
            "bq": bf(np.random.standard_normal(DIM) * 0.3),
            "bk": bf(np.random.standard_normal(DIM) * 0.3),
            "gq": bf(1.5 + 0.15 * np.random.standard_normal(DIM)),
            "gk": bf(1.5 + 0.15 * np.random.standard_normal(DIM)),
            "freqs_cos": bf(np.cos(ang)),
            "freqs_sin": bf(np.sin(ang))}


def reference(x, wq_words, wq_scales, wk_words, wk_scales, bq, bk, gq, gk, freqs_cos, freqs_sin):
    xq = mxq(f64(x), 2, "e5m2")
    q = rms((xq @ unpack4(wq_words, wq_scales)) + f64(bq), f64(gq))
    k = rms((xq @ unpack4(wk_words, wk_scales)) + f64(bk), f64(gk))
    cos, sin = f64(freqs_cos), f64(freqs_sin)
    return rope(q, cos, sin), rope(k, cos, sin)

@@ -1,0 +1,435 @@
+from contextlib import ExitStack
+
+import concourse.mybir as mybir
+from concourse.masks import make_identity
+
+L, D, NH, HD = 1024, 1536, 12, 128
+EPS = 1e-6
+FLOPS = 2 * 2 * L * D * D
+
+F32 = mybir.dt.float32
+BF16 = mybir.dt.bfloat16
+I32 = mybir.dt.int32
+U32 = mybir.dt.uint32
+U8 = mybir.dt.uint8
+FP8X4 = mybir.dt.float8_e5m2_x4
+FP4X4 = mybir.dt.float4_e2m1fn_x4
+ALU = mybir.AluOpType
+ACT = mybir.ActivationFunctionType
+AXIS = mybir.AxisListType
+
+P = 128
+PASSES = D // 512
+QUAD = 4
+NT = L // P
+
+CHUNKS = [(0, 2), (2, 2), (4, 4)]
+GROUPS = [(0, 0, 0, 2, 6, False), (1, 0, 0, 2, 1, False), (0, 1, 2, 2, 1, False), (1, 1, 2, 2, 1, False), (0, 2, 4, 2, 1, False), (1, 2, 4, 2, 1, False), (0, 2, 6, 2, 1, False), (1, 2, 6, 1, 1, False), (1, 2, 7, 1, 1, False)]
+K_EARLY = True
+STEP = 2
+T_BANKS = 4
+MX_BANKS = 3
+SQ_BUFS = 8
+W_BUFS = 16
+T1_BUFS = 8
+T2_BUFS = 4
+UNITS_PER_STEP = 2
+BACKLOG = 2
+X_START = 1
+X_PER_STEP = 1
+X_ON_SCALAR = False
+TAIL_GROUPS = 1
+V_ADD_GROUPS = 1
+LATE_SPLIT = 1024
+V_ADD_UNITS = 2
+SCALES_PER_STEP = 1
+TAIL_SPLIT = 512
+SCALE_DELAY = 2
+V_ADD_EVERY = 100
+SQRT_AT = 2
+
+
+def tile_causalwanselfattention_pa_kernel(
+    tc, x, wq_words, wq_scales, wk_words, wk_scales, bq, bk, gq, gk, freqs_cos, freqs_sin, out_0, out_1
+):
+    nc = tc.nc
+    x2 = x.rearrange("b l d -> (b l) d")
+    outs = [o.rearrange("b l h d -> (b l) (h d)") for o in (out_0, out_1)]
+    words_in = (wq_words, wk_words)
+    scales_in = (wq_scales, wk_scales)
+
+    with ExitStack() as ctx:
+        keep = ctx.enter_context(tc.tile_pool(name="keep", bufs=1))
+        work = ctx.enter_context(tc.tile_pool(name="work", bufs=1))
+        psum = ctx.enter_context(tc.psum_pool(name="psum", bufs=1))
+        ctx.enter_context(tc.manual_schedule())
+
+        ident = keep.tile([P, P], F32, name="ident")
+        make_identity(nc, ident[:])
+
+        planes = []
+        for proj in range(2):
+            plane = keep.tile([P, PASSES, D], U8, name="wplane%d" % proj, align_bytes=64)
+            planes.append(plane)
+        rows32 = keep.tile([P, P], F32, name="rows32")
+        nc.vector.memset(planes[0][:].rearrange("p g n -> p (g n)").bitcast(I32), 0)
+        nc.vector.memset(rows32[:], 0.0)
+        nc.vector.memset(planes[1][:].rearrange("p g n -> p (g n)").bitcast(I32), 0)
+
+        xraw = {}
+
+        def load_x(chunk, g):
+            t0, nt = CHUNKS[chunk]
+            t = keep.tile([P, nt, 512], BF16, name="xraw%d_%d" % (chunk, g))
+            nc.sync.dma_start(
+                out=t[:],
+                in_=x2[t0 * P : (t0 + nt) * P, g * 512 : (g + 1) * 512].rearrange("(t p) k -> p t k", p=P),
+            )
+            xraw[chunk, g] = t
+
+        def load_scales(proj):
+            for q in range(4):
+                nc.sync.dma_start(
+                    out=planes[proj][32 * q : 32 * q + 4, :, :].bitcast(I32),
+                    in_=scales_in[proj][:, 4 * q : 4 * q + 4, :].rearrange("g r n -> r g n").bitcast(I32),
+                )
+
+        wcodes = {}
+
+        def load_w(proj, h0, h1):
+            t = keep.tile([P, PASSES, (h1 - h0) * 2 * HD], U8, name="w%d_%d" % (proj, h0), align_bytes=64)
+            nc.sync.dma_start(
+                out=t[:].bitcast(I32),
+                in_=words_in[proj][:, :, h0 * 2 * HD : h1 * 2 * HD].rearrange("g p n -> p g n").bitcast(I32),
+            )
+            for h in range(h0, h1):
+                wcodes[proj, h] = (t, h - h0)
+
+        rows16 = keep.tile([4 * NH, HD], BF16, name="rows16")
+        for i, vec in enumerate((bq, bk, gq, gk)):
+            nc.gpsimd.dma_start(out=rows16[i * NH : (i + 1) * NH, :], in_=vec.rearrange("(h d) -> h d", d=HD))
+
+        cos_in = keep.tile([P, NT, HD // 2], BF16, name="cos_in")
+        sin_in = keep.tile([P, NT, HD // 2], BF16, name="sin_in")
+
+        for g in range(PASSES):
+            load_x(0, g)
+        load_scales(0)
+        load_w(0, 0, 4)
+        load_w(0, 4, NH)
+        nc.sync.dma_start(out=cos_in[:], in_=freqs_cos.rearrange("(t p) c -> p t c", p=P))
+        nc.sync.dma_start(out=sin_in[:], in_=freqs_sin.rearrange("(t p) c -> p t c", p=P))
+        if K_EARLY:
+            load_scales(1)
+            load_w(1, 0, NH)
+        for chunk in range(1, len(CHUNKS)):
+            for g in range(PASSES):
+                load_x(chunk, g)
+            if chunk == 1 and not K_EARLY:
+                load_scales(1)
+                load_w(1, 0, NH)
+
+        xcodes, xscales, grouped = {}, {}, {}
+        for chunk, (t0, nt) in enumerate(CHUNKS):
+            xcodes[chunk] = keep.tile([P, PASSES, nt * P], U32, name="xc%d" % chunk, align_bytes=64)
+            xscales[chunk] = keep.tile([P, PASSES, nt * P], U8, name="xs%d" % chunk, align_bytes=64)
+
+        def x_transpose(chunk, g, j0):
+            nt = CHUNKS[chunk][1]
+            nj = min(2, nt - j0)
+            bank = psum.tile([P, nj, 2, P], F32, name="xbank", tag="tbank", bufs=T_BANKS)
+            words = xraw[chunk, g][:].bitcast(F32)
+            for j in range(nj):
+                for u in range(2):
+                    nc.tensor.transpose(bank[:, j, u, :], words[:, j0 + j, u : 256 : 2], ident[:])
+            return bank
+
+        def x_copy(chunk, g, j0, bank, on_scalar):
+            nt = CHUNKS[chunk][1]
+            nj = min(2, nt - j0)
+            if j0 == 0:
+                grouped[chunk, g] = work.tile([P, nt * P * 4], BF16, name="grouped", tag="grouped", bufs=3, align_bytes=64)
+            dst = grouped[chunk, g][:].bitcast(F32)[:, j0 * 256 : (j0 + nj) * 256].rearrange("p (j r u) -> p j r u", j=nj, u=2)
+            src = bank[:].rearrange("p j u r -> p j r u")
+            if on_scalar:
+                nc.scalar.copy(out=dst, in_=src)
+            else:
+                nc.vector.tensor_copy(out=dst, in_=src)
+
+        def x_quantize(chunk, g):
+            nc.vector.quantize_mx(
+                out=xcodes[chunk][:, g, :].bitcast(FP8X4), scales=xscales[chunk][:, g, :], in_=grouped[chunk, g][:]
+            )
+
+        x_items = [
+            (chunk, g, j0) for chunk in range(len(CHUNKS)) for g in range(PASSES) for j0 in range(0, CHUNKS[chunk][1], 2)
+        ]
+
+        cols = keep.tile([P, 4 * NH], F32, name="cols")
+        gb = keep.tile([P, 2 * NH], F32, name="gb")
+
+        def params():
+            nc.vector.tensor_copy(out=rows32[0 : 4 * NH, :], in_=rows16[:])
+            pbank = psum.tile([P, P], F32, name="pbank", tag="ssbank", bufs=1)
+            nc.tensor.transpose(pbank[:], rows32[:], ident[:])
+            nc.vector.tensor_copy(out=cols[:], in_=pbank[:, 0 : 4 * NH])
+            nc.vector.tensor_tensor(out=gb[:], in0=cols[:, 0 : 2 * NH], in1=cols[:, 2 * NH : 4 * NH], op=ALU.mult)
+
+        cos2 = keep.tile([P, NT, HD // 2, 2], BF16, name="cos2")
+        sin2 = keep.tile([P, NT, HD // 2, 2], BF16, name="sin2")
+
+        def tables():
+            shape = [P, NT * HD // 2, 2]
+            sign = keep.tile([P, 1, 2], F32, name="sign")
+            nc.vector.memset(sign[:, :, 0:1], -1.0)
+            nc.vector.memset(sign[:, :, 1:2], 1.0)
+            nc.vector.tensor_copy(
+                out=cos2[:].rearrange("p t c e -> p (t c) e"),
+                in_=cos_in[:].rearrange("p t (c e) -> p (t c) e", e=1).to_broadcast(shape),
+            )
+            nc.vector.tensor_tensor(
+                out=sin2[:].rearrange("p t c e -> p (t c) e"),
+                in0=sin_in[:].rearrange("p t (c e) -> p (t c) e", e=1).to_broadcast(shape),
+                in1=sign[:].to_broadcast(shape),
+                op=ALU.mult,
+            )
+
+        first = [it for it in x_items if it[0] == 0]
+        later = [it for it in x_items if it[0] != 0]
+        waiting_q = None
+        for i, (chunk, g, j0) in enumerate(first):
+            bank = x_transpose(chunk, g, j0)
+            x_copy(chunk, g, j0, bank, on_scalar=(i % 2 == 1) or CHUNKS[0][1] <= 2)
+            if j0 + 2 >= CHUNKS[chunk][1]:
+                x_quantize(chunk, g)
+
+        state = {}
+
+        def job_heads(gi, job):
+            hb = QUAD // GROUPS[gi][3]
+            return range(job * hb, (job + 1) * hb)
+
+        def mx_job(gi, job):
+            proj, chunk, t0, nt = GROUPS[gi][:4]
+            c0 = (t0 - CHUNKS[chunk][0]) * P
+            n = nt * P
+            acc = psum.tile([P, QUAD // nt, n], F32, name="acc", tag="acc", bufs=MX_BANKS)
+            for i, h in enumerate(job_heads(gi, job)):
+                wt, hl = wcodes[proj, h]
+                for g in range(PASSES):
+                    nc.tensor.matmul_mx(
+                        out=acc[:, i, :],
+                        lhsT=wt[:, g, hl * 2 * HD : (hl + 1) * 2 * HD].bitcast(FP4X4),
+                        lhsT_scale=planes[proj][:, g, h * HD : (h + 1) * HD],
+                        rhs=xcodes[chunk][:, g, c0 : c0 + n].bitcast(FP8X4),
+                        rhs_scale=xscales[chunk][:, g, c0 : c0 + n],
+                        start=(g == 0),
+                        stop=(g == PASSES - 1),
+                    )
+            return acc
+
+        def drain_job(gi, job, acc):
+            proj, chunk, t0, nt = GROUPS[gi][:4]
+            sq = work.tile([P, QUAD * P], F32, name="sq", tag="sq", bufs=SQ_BUFS)
+            w = work.tile([P, QUAD * P], F32, name="w", tag="w", bufs=W_BUFS)
+            n = nt * P
+            for i, h in enumerate(job_heads(gi, job)):
+                col = proj * NH + h
+                nc.scalar.activation(
+                    out=sq[:, i * n : (i + 1) * n], in_=acc[:, i, :], func=ACT.Square, bias=cols[:, col : col + 1]
+                )
+            for i, h in enumerate(job_heads(gi, job)):
+                col = proj * NH + h
+                nc.scalar.activation(
+                    out=w[:, i * n : (i + 1) * n], in_=acc[:, i, :], func=ACT.Identity,
+                    scale=cols[:, 2 * NH + col : 2 * NH + col + 1], bias=gb[:, col : col + 1],
+                )
+                state["w", gi, h] = w[:, i * n : (i + 1) * n]
+            return sq
+
+        def ss_transpose(gi, sq, first_one, last_one):
+            nt = GROUPS[gi][3]
+            if first_one:
+                state["ss", gi] = psum.tile([P, nt, P], F32, name="ss", tag="ssbank", bufs=1)
+            bank = state["ss", gi]
+            for b in range(QUAD):
+                nc.tensor.matmul(
+                    out=bank[:, b % nt, :], lhsT=sq[:, b * P : (b + 1) * P], rhs=ident[:],
+                    start=(first_one and b == 0), stop=(last_one and b == QUAD - 1), is_transpose=True,
+                )
+
+        def ss_reduce(gi):
+            nt = GROUPS[gi][3]
+            total = work.tile([P, nt], F32, name="total", tag="total", bufs=2)
+            nc.vector.tensor_reduce(out=total[:], in_=state["ss", gi][:], axis=AXIS.X, op=ALU.add)
+            state["total", gi] = total
+
+        def ss_sqrt(gi):
+            nt = GROUPS[gi][3]
+            root = work.tile([P, nt], F32, name="root", tag="root", bufs=2)
+            nc.scalar.activation(out=root[:], in_=state["total", gi][:], func=ACT.Sqrt, scale=1.0 / D, bias=EPS)
+            state["root", gi] = root
+
+        def ss_recip(gi):
+            nt = GROUPS[gi][3]
+            rstd = work.tile([P, nt], F32, name="rstd", tag="rstd", bufs=3)
+            nc.vector.reciprocal(out=rstd[:], in_=state["root", gi][:])
+            state["rstd", gi] = rstd
+
+        def unit_transpose(gi, t, hq):
+            bank = psum.tile([P, QUAD, HD], F32, name="wbank", tag="tbank", bufs=T_BANKS)
+            for i in range(QUAD):
+                w = state["w", gi, hq * QUAD + i]
+                nc.tensor.transpose(bank[:, i, :], w[:, t * P : (t + 1) * P], ident[:])
+            return bank
+
+        def store(gi, t, cs):
+            proj, chunk, t0 = GROUPS[gi][:3]
+            nc.sync.dma_start(out=outs[proj][(t0 + t) * P : (t0 + t + 1) * P, cs], in_=state["y", gi, t][:, cs])
+
+        def unit_rotate(gi, t, hq, bank):
+            proj, chunk, t0, nt, fold, late = GROUPS[gi]
+            if ("y", gi, t) not in state:
+                state["y", gi, t] = work.tile([P, D], F32, name="y", tag="y", bufs=T1_BUFS)
+                state["done", gi, t] = 0
+            y = state["y", gi, t]
+            t2 = work.tile([P, QUAD * HD], F32, name="t2", tag="t2", bufs=T2_BUFS)
+            cs = slice(hq * QUAD * HD, (hq + 1) * QUAD * HD)
+            pairs = bank[:].rearrange("p h (c e) -> p h c e", e=2)
+            shape = [P, QUAD, HD // 2, 2]
+            ctab = cos2[:, t0 + t : t0 + t + 1, :, :].to_broadcast(shape)
+            stab = sin2[:, t0 + t : t0 + t + 1, :, :].to_broadcast(shape)
+            o1 = y[:, cs].rearrange("p (h c e) -> p h c e", h=QUAD, e=2)
+            o2 = t2[:].rearrange("p (h c e) -> p h c e", h=QUAD, e=2)
+            if late:
+                nc.vector.tensor_tensor(out=o1, in0=pairs, in1=ctab, op=ALU.mult)
+                nc.vector.tensor_tensor(out=o2, in0=pairs[:, :, :, ::-1], in1=stab, op=ALU.mult)
+            else:
+                r = state["rstd", gi][:, t : t + 1]
+                nc.vector.scalar_tensor_tensor(out=o1, in0=pairs, scalar=r, in1=ctab, op0=ALU.mult, op1=ALU.mult)
+                nc.vector.scalar_tensor_tensor(
+                    out=o2, in0=pairs[:, :, :, ::-1], scalar=r, in1=stab, op0=ALU.mult, op1=ALU.mult
+                )
+            state["count"] = state.get("count", 0) + 1
+            on_vector = state["count"] > NT * 2 * NH // QUAD - V_ADD_UNITS or state["count"] % V_ADD_EVERY == 0
+            adder = nc.vector if on_vector else nc.gpsimd
+            state["adds"].append((adder, y[:, cs], t2))
+            state["done", gi, t] += 1
+            complete = state["done", gi, t] == NH // QUAD
+            if late:
+                if complete:
+                    state["scale"].append((gi, t, state["si"] + SCALE_DELAY))
+            elif gi >= len(GROUPS) - TAIL_GROUPS:
+                state["stores"].append((gi, t, cs))
+            elif complete:
+                state["stores"].append((gi, t, slice(0, D)))
+
+        def flush_adds():
+            for adder, ycs, t2 in state["adds"]:
+                adder.tensor_tensor(out=ycs, in0=ycs, in1=t2[:], op=ALU.add)
+            state["adds"] = []
+            for e in state["stores"]:
+                store(*e)
+            state["stores"] = []
+
+        def late_scale(entries):
+            for gi, t, due in entries:
+                y = state["y", gi, t]
+                r = state["rstd", gi][:, t : t + 1]
+                split = LATE_SPLIT if gi < len(GROUPS) - TAIL_GROUPS else TAIL_SPLIT
+                nc.scalar.activation(out=y[:, :split], in_=y[:, :split], func=ACT.Copy, scale=r)
+                if split < D:
+                    if gi < len(GROUPS) - TAIL_GROUPS:
+                        nc.gpsimd.tensor_scalar(out=y[:, split:], in0=y[:, split:], scalar1=r, scalar2=0.0, op0=ALU.mult, op1=ALU.add)
+                    else:
+                        nc.vector.tensor_scalar(out=y[:, split:], in0=y[:, split:], scalar1=r, scalar2=None, op0=ALU.mult)
+                if gi < len(GROUPS) - TAIL_GROUPS:
+                    store(gi, t, slice(0, D))
+                else:
+                    store(gi, t, slice(split, D))
+                    store(gi, t, slice(0, split))
+
+        state["adds"], state["stores"], state["scale"] = [], [], []
+        steps = []
+        for gi in range(len(GROUPS)):
+            jobs = NH * GROUPS[gi][3] // QUAD
+            steps.extend((gi, list(range(j, min(j + STEP, jobs)))) for j in range(0, jobs, STEP))
+        units = []
+        sq_ready = []
+        folding = {}
+        for si in range(len(steps) + 1):
+            live = si < len(steps)
+            state["si"] = si
+            accs = []
+            if live:
+                gi, jobs = steps[si]
+                for job in jobs:
+                    accs.append((job, mx_job(gi, job)))
+            if si == 0:
+                params()
+            closing = []
+            for cgi, sq, first_one, last_one, due in sq_ready:
+                if due <= si:
+                    ss_transpose(cgi, sq, first_one, last_one)
+                    if last_one:
+                        closing.append(cgi)
+            sq_ready = [e for e in sq_ready if e[4] > si]
+            xs = []
+            if live and later and si >= X_START:
+                for it in later[:X_PER_STEP]:
+                    xs.append((it, x_transpose(*it)))
+                later = later[X_PER_STEP:]
+            take = min(UNITS_PER_STEP + (1 if len(units) > BACKLOG else 0), T_BANKS - len(xs))
+            now = units[:take]
+            units = units[take:]
+            banks = [unit_transpose(*u) for u in now]
+            for cgi in closing:
+                ss_reduce(cgi)
+            new_sq = []
+            for i, (job, acc) in enumerate(accs):
+                new_sq.append((job, drain_job(gi, job, acc)))
+                if i == min(SQRT_AT, len(accs) - 1):
+                    for cgi in closing:
+                        ss_sqrt(cgi)
+            if not accs:
+                for cgi in closing:
+                    ss_sqrt(cgi)
+            ready = [e for e in state["scale"] if e[2] <= si and state.get(("rstd_step", e[0]), si) < si][:SCALES_PER_STEP]
+            late_scale(ready)
+            state["scale"] = [e for e in state["scale"] if e not in ready]
+            if si == 0:
+                tables()
+            for it, bank in xs:
+                x_copy(it[0], it[1], it[2], bank, on_scalar=X_ON_SCALAR)
+            for u, bank in zip(now, banks):
+                unit_rotate(u[0], u[1], u[2], bank)
+            flush_adds()
+            for it, bank in xs:
+                if it[2] + 2 >= CHUNKS[it[0]][1]:
+                    x_quantize(it[0], it[1])
+            for cgi in closing:
+                ss_recip(cgi)
+                state["rstd_step", cgi] = si
+                if not GROUPS[cgi][5]:
+                    units.extend((cgi, t, hq) for t in range(GROUPS[cgi][3]) for hq in range(NH // QUAD))
+            for job, sq in new_sq:
+                nt, fold, late = GROUPS[gi][3:6]
+                njobs = NH * nt // QUAD
+                if job % fold == 0:
+                    folding[gi] = sq
+                else:
+                    acc_sq = work.tile([P, QUAD * P], F32, name="sqsum", tag="sqsum", bufs=3)
+                    nc.vector.tensor_tensor(out=acc_sq[:], in0=folding[gi][:], in1=sq[:], op=ALU.add)
+                    folding[gi] = acc_sq
+                if job % fold == fold - 1 or job == njobs - 1:
+                    sq_ready.append((gi, folding[gi], job < fold, job == njobs - 1, si + (2 if fold > 1 else 1)))
+                if late and (job + 1) % nt == 0:
+                    units.extend((gi, t, job // nt) for t in range(nt))
+        while units:
+            now = units[:2]
+            units = units[2:]
+            banks = [unit_transpose(*u) for u in now]
+            for u, bank in zip(now, banks):
+                unit_rotate(u[0], u[1], u[2], bank)
+                flush_adds()
+        late_scale(state["scale"])

@@ -24,29 +24,24 @@ QUAD = 4
 NT = L // P
 
 CHUNKS = [(0, 2), (2, 2), (4, 4)]
-GROUPS = [(0, 0, 0, 2, 6, False), (1, 0, 0, 2, 1, False), (0, 1, 2, 2, 1, False), (1, 1, 2, 2, 1, False), (0, 2, 4, 2, 1, False), (1, 2, 4, 2, 1, False), (0, 2, 6, 2, 1, False), (1, 2, 6, 1, 1, False), (1, 2, 7, 1, 1, False)]
-K_EARLY = True
+GROUPS = [(0, 0, 2, 0, 2), (0, 2, 2, 0, 2), (1, 0, 4, 0, 2), (0, 4, 4, 0, 2), (1, 4, 4, 2, 1)]
+K_BEFORE = 2
 STEP = 2
-T_BANKS = 4
+T_BANKS = 3
 MX_BANKS = 3
 SQ_BUFS = 8
-W_BUFS = 16
-T1_BUFS = 8
-T2_BUFS = 4
+W_BUFS = 5
+PROD_BUFS = 42
+Y_BUFS = 8
 UNITS_PER_STEP = 2
-BACKLOG = 2
-X_START = 1
-X_PER_STEP = 1
-X_ON_SCALAR = False
-TAIL_GROUPS = 1
-V_ADD_GROUPS = 1
-LATE_SPLIT = 1024
-V_ADD_UNITS = 2
-SCALES_PER_STEP = 1
-TAIL_SPLIT = 512
-SCALE_DELAY = 2
-V_ADD_EVERY = 100
-SQRT_AT = 2
+X_START = 0
+X_PER_STEP = 2
+X_ON_SCALAR = 1
+V_EVERY = 2
+UNIT_DELAY = 2
+V_NUM = 1
+TAIL_TAKE = 4
+K_PARAMS = 4
 
 
 def tile_causalwanselfattention_pa_kernel(
@@ -71,10 +66,13 @@ def tile_causalwanselfattention_pa_kernel(
         for proj in range(2):
             plane = keep.tile([P, PASSES, D], U8, name="wplane%d" % proj, align_bytes=64)
             planes.append(plane)
-        rows32 = keep.tile([P, P], F32, name="rows32")
+        rows32 = [keep.tile([P, P], F32, name="rows32_%d" % proj) for proj in range(2)]
+        minus_half = keep.tile([P, 4], F32, name="minus_half")
         nc.vector.memset(planes[0][:].rearrange("p g n -> p (g n)").bitcast(I32), 0)
-        nc.vector.memset(rows32[:], 0.0)
+        nc.vector.memset(rows32[0][:], 0.0)
         nc.vector.memset(planes[1][:].rearrange("p g n -> p (g n)").bitcast(I32), 0)
+        nc.vector.memset(rows32[1][:], 0.0)
+        nc.vector.memset(minus_half[:], -0.5)
 
         xraw = {}
 
@@ -105,9 +103,13 @@ def tile_causalwanselfattention_pa_kernel(
             for h in range(h0, h1):
                 wcodes[proj, h] = (t, h - h0)
 
-        rows16 = keep.tile([4 * NH, HD], BF16, name="rows16")
-        for i, vec in enumerate((bq, bk, gq, gk)):
-            nc.gpsimd.dma_start(out=rows16[i * NH : (i + 1) * NH, :], in_=vec.rearrange("(h d) -> h d", d=HD))
+        rows16 = [keep.tile([2 * NH, HD], BF16, name="rows16_%d" % proj) for proj in range(2)]
+
+        def load_rows(queue, proj):
+            for i, vec in enumerate(((bq, gq), (bk, gk))[proj]):
+                queue.dma_start(out=rows16[proj][i * NH : (i + 1) * NH, :], in_=vec.rearrange("(h d) -> h d", d=HD))
+
+        load_rows(nc.scalar, 0)
 
         cos_in = keep.tile([P, NT, HD // 2], BF16, name="cos_in")
         sin_in = keep.tile([P, NT, HD // 2], BF16, name="sin_in")
@@ -116,23 +118,22 @@ def tile_causalwanselfattention_pa_kernel(
             load_x(0, g)
         load_scales(0)
         load_w(0, 0, 4)
-        load_w(0, 4, NH)
         nc.sync.dma_start(out=cos_in[:], in_=freqs_cos.rearrange("(t p) c -> p t c", p=P))
         nc.sync.dma_start(out=sin_in[:], in_=freqs_sin.rearrange("(t p) c -> p t c", p=P))
-        if K_EARLY:
-            load_scales(1)
-            load_w(1, 0, NH)
+        load_w(0, 4, NH)
         for chunk in range(1, len(CHUNKS)):
-            for g in range(PASSES):
-                load_x(chunk, g)
-            if chunk == 1 and not K_EARLY:
+            if chunk == K_BEFORE:
                 load_scales(1)
                 load_w(1, 0, NH)
+                load_rows(nc.sync, 1)
+            for g in range(PASSES):
+                load_x(chunk, g)
 
         xcodes, xscales, grouped = {}, {}, {}
-        for chunk, (t0, nt) in enumerate(CHUNKS):
-            xcodes[chunk] = keep.tile([P, PASSES, nt * P], U32, name="xc%d" % chunk, align_bytes=64)
-            xscales[chunk] = keep.tile([P, PASSES, nt * P], U8, name="xs%d" % chunk, align_bytes=64)
+        for half in range(2):
+            for g in range(PASSES):
+                xcodes[half, g] = keep.tile([P, 512], U32, name="xc%d_%d" % (half, g), align_bytes=64)
+                xscales[half, g] = keep.tile([P, 512], U8, name="xs%d_%d" % (half, g), align_bytes=64)
 
         def x_transpose(chunk, g, j0):
             nt = CHUNKS[chunk][1]
@@ -157,32 +158,40 @@ def tile_causalwanselfattention_pa_kernel(
                 nc.vector.tensor_copy(out=dst, in_=src)
 
         def x_quantize(chunk, g):
+            t0, nt = CHUNKS[chunk]
+            cs = slice(t0 % 4 * P, (t0 % 4 + nt) * P)
             nc.vector.quantize_mx(
-                out=xcodes[chunk][:, g, :].bitcast(FP8X4), scales=xscales[chunk][:, g, :], in_=grouped[chunk, g][:]
+                out=xcodes[t0 // 4, g][:, cs].bitcast(FP8X4), scales=xscales[t0 // 4, g][:, cs], in_=grouped[chunk, g][:]
             )
 
         x_items = [
             (chunk, g, j0) for chunk in range(len(CHUNKS)) for g in range(PASSES) for j0 in range(0, CHUNKS[chunk][1], 2)
         ]
 
-        cols = keep.tile([P, 4 * NH], F32, name="cols")
-        gb = keep.tile([P, 2 * NH], F32, name="gb")
+        cols = [keep.tile([P, 2 * NH], F32, name="cols%d" % proj) for proj in range(2)]
+        gb = [keep.tile([P, NH], F32, name="gb%d" % proj) for proj in range(2)]
 
-        def params():
-            nc.vector.tensor_copy(out=rows32[0 : 4 * NH, :], in_=rows16[:])
-            pbank = psum.tile([P, P], F32, name="pbank", tag="ssbank", bufs=1)
-            nc.tensor.transpose(pbank[:], rows32[:], ident[:])
-            nc.vector.tensor_copy(out=cols[:], in_=pbank[:, 0 : 4 * NH])
-            nc.vector.tensor_tensor(out=gb[:], in0=cols[:, 0 : 2 * NH], in1=cols[:, 2 * NH : 4 * NH], op=ALU.mult)
+        def widen_rows(proj):
+            nc.vector.tensor_copy(out=rows32[proj][0 : 2 * NH, :], in_=rows16[proj][:])
 
-        cos2 = keep.tile([P, NT, HD // 2, 2], BF16, name="cos2")
-        sin2 = keep.tile([P, NT, HD // 2, 2], BF16, name="sin2")
+        def params(proj):
+            pbank = psum.tile([P, P], F32, name="pbank", tag="tbank", bufs=T_BANKS)
+            nc.tensor.transpose(pbank[:], rows32[proj][:], ident[:])
+            nc.vector.tensor_copy(out=cols[proj][:], in_=pbank[:, 0 : 2 * NH])
+            nc.vector.tensor_tensor(out=gb[proj][:], in0=cols[proj][:, 0:NH], in1=cols[proj][:, NH : 2 * NH], op=ALU.mult)
+
+        cos2 = keep.tile([P, NT, HD // 2, 2], F32, name="cos2")
+        sin2 = keep.tile([P, NT, HD // 2, 2], F32, name="sin2")
+        swap = keep.tile([P, P], F32, name="swap")
 
         def tables():
             shape = [P, NT * HD // 2, 2]
+            nc.vector.tensor_copy(
+                out=swap[:].rearrange("p (c e) -> p c e", e=2), in_=ident[:].rearrange("p (c e) -> p c e", e=2)[:, :, ::-1]
+            )
             sign = keep.tile([P, 1, 2], F32, name="sign")
-            nc.vector.memset(sign[:, :, 0:1], -1.0)
-            nc.vector.memset(sign[:, :, 1:2], 1.0)
+            nc.vector.memset(sign[:, :, 0:1], 1.0)
+            nc.vector.memset(sign[:, :, 1:2], -1.0)
             nc.vector.tensor_copy(
                 out=cos2[:].rearrange("p t c e -> p (t c) e"),
                 in_=cos_in[:].rearrange("p t (c e) -> p (t c) e", e=1).to_broadcast(shape),
@@ -196,24 +205,32 @@ def tile_causalwanselfattention_pa_kernel(
 
         first = [it for it in x_items if it[0] == 0]
         later = [it for it in x_items if it[0] != 0]
-        waiting_q = None
+        widen_rows(0)
         for i, (chunk, g, j0) in enumerate(first):
             bank = x_transpose(chunk, g, j0)
             x_copy(chunk, g, j0, bank, on_scalar=(i % 2 == 1) or CHUNKS[0][1] <= 2)
+            if i == len(first) - 1:
+                params(0)
             if j0 + 2 >= CHUNKS[chunk][1]:
                 x_quantize(chunk, g)
 
         state = {}
 
         def job_heads(gi, job):
-            hb = QUAD // GROUPS[gi][3]
+            hb = QUAD // GROUPS[gi][2]
             return range(job * hb, (job + 1) * hb)
 
+        def table_transpose(half):
+            for name, src in (("cosT", cos2), ("sinT", sin2)):
+                bank = psum.tile([P, 4, P], F32, name=name, tag=name, bufs=1)
+                for t in range(4):
+                    nc.tensor.transpose(bank[:, t, :], src[:, half * 4 + t, :, :].rearrange("p c e -> p (c e)"), ident[:])
+                state[name, half] = bank
+
         def mx_job(gi, job):
-            proj, chunk, t0, nt = GROUPS[gi][:4]
-            c0 = (t0 - CHUNKS[chunk][0]) * P
-            n = nt * P
-            acc = psum.tile([P, QUAD // nt, n], F32, name="acc", tag="acc", bufs=MX_BANKS)
+            proj, t0, nt = GROUPS[gi][:3]
+            cs = slice(t0 % 4 * P, (t0 % 4 + nt) * P)
+            acc = psum.tile([P, QUAD // nt, nt * P], F32, name="acc", tag="acc", bufs=MX_BANKS)
             for i, h in enumerate(job_heads(gi, job)):
                 wt, hl = wcodes[proj, h]
                 for g in range(PASSES):
@@ -221,215 +238,171 @@ def tile_causalwanselfattention_pa_kernel(
                         out=acc[:, i, :],
                         lhsT=wt[:, g, hl * 2 * HD : (hl + 1) * 2 * HD].bitcast(FP4X4),
                         lhsT_scale=planes[proj][:, g, h * HD : (h + 1) * HD],
-                        rhs=xcodes[chunk][:, g, c0 : c0 + n].bitcast(FP8X4),
-                        rhs_scale=xscales[chunk][:, g, c0 : c0 + n],
+                        rhs=xcodes[t0 // 4, g][:, cs].bitcast(FP8X4),
+                        rhs_scale=xscales[t0 // 4, g][:, cs],
                         start=(g == 0),
                         stop=(g == PASSES - 1),
                     )
             return acc
 
         def drain_job(gi, job, acc):
-            proj, chunk, t0, nt = GROUPS[gi][:4]
+            proj, t0, nt = GROUPS[gi][:3]
             sq = work.tile([P, QUAD * P], F32, name="sq", tag="sq", bufs=SQ_BUFS)
             w = work.tile([P, QUAD * P], F32, name="w", tag="w", bufs=W_BUFS)
             n = nt * P
             for i, h in enumerate(job_heads(gi, job)):
-                col = proj * NH + h
-                nc.scalar.activation(
-                    out=sq[:, i * n : (i + 1) * n], in_=acc[:, i, :], func=ACT.Square, bias=cols[:, col : col + 1]
-                )
-            for i, h in enumerate(job_heads(gi, job)):
-                col = proj * NH + h
                 nc.scalar.activation(
                     out=w[:, i * n : (i + 1) * n], in_=acc[:, i, :], func=ACT.Identity,
-                    scale=cols[:, 2 * NH + col : 2 * NH + col + 1], bias=gb[:, col : col + 1],
+                    scale=cols[proj][:, NH + h : NH + h + 1], bias=gb[proj][:, h : h + 1],
                 )
-                state["w", gi, h] = w[:, i * n : (i + 1) * n]
-            return sq
+            for i, h in enumerate(job_heads(gi, job)):
+                nc.scalar.activation(
+                    out=sq[:, i * n : (i + 1) * n], in_=acc[:, i, :], func=ACT.Square, bias=cols[proj][:, h : h + 1]
+                )
+            return w, sq
 
-        def ss_transpose(gi, sq, first_one, last_one):
-            nt = GROUPS[gi][3]
-            if first_one:
-                state["ss", gi] = psum.tile([P, nt, P], F32, name="ss", tag="ssbank", bufs=1)
-            bank = state["ss", gi]
-            for b in range(QUAD):
-                nc.tensor.matmul(
-                    out=bank[:, b % nt, :], lhsT=sq[:, b * P : (b + 1) * P], rhs=ident[:],
-                    start=(first_one and b == 0), stop=(last_one and b == QUAD - 1), is_transpose=True,
+        def rotate_job(gi, job, w):
+            proj, t0, nt = GROUPS[gi][:3]
+            hb, n = QUAD // nt, nt * P
+            for name in ("cosT", "sinT"):
+                tab = state[name, t0 // 4][:, t0 % 4 : t0 % 4 + nt, :].rearrange("p (o t) l -> p o (t l)", o=1)
+                prod = work.tile([P, hb, n], F32, name="prod", tag="prod", bufs=PROD_BUFS)
+                nc.vector.tensor_tensor(
+                    out=prod[:], in0=w[:].rearrange("p (h l) -> p h l", h=hb), in1=tab.to_broadcast([P, hb, n]), op=ALU.mult
                 )
+                for i, h in enumerate(job_heads(gi, job)):
+                    state[name, gi, h] = prod[:, i, :]
+
+        def ss_transpose(gi, parts):
+            nt = GROUPS[gi][2]
+            bank = psum.tile([P, nt, P], F32, name="ss", tag="tbank", bufs=T_BANKS)
+            for t in range(nt):
+                blocks = [sq[:, b * P : (b + 1) * P] for sq in parts for b in range(t, QUAD, nt)]
+                for i, blk in enumerate(blocks):
+                    nc.tensor.matmul(
+                        out=bank[:, t, :], lhsT=blk, rhs=ident[:],
+                        start=(i == 0), stop=(i == len(blocks) - 1), is_transpose=True,
+                    )
+            state["ss", gi] = bank
 
         def ss_reduce(gi):
-            nt = GROUPS[gi][3]
+            nt = GROUPS[gi][2]
             total = work.tile([P, nt], F32, name="total", tag="total", bufs=2)
             nc.vector.tensor_reduce(out=total[:], in_=state["ss", gi][:], axis=AXIS.X, op=ALU.add)
             state["total", gi] = total
 
-        def ss_sqrt(gi):
-            nt = GROUPS[gi][3]
-            root = work.tile([P, nt], F32, name="root", tag="root", bufs=2)
-            nc.scalar.activation(out=root[:], in_=state["total", gi][:], func=ACT.Sqrt, scale=1.0 / D, bias=EPS)
-            state["root", gi] = root
-
-        def ss_recip(gi):
-            nt = GROUPS[gi][3]
+        def ss_rstd(gi):
+            nt = GROUPS[gi][2]
+            var = work.tile([P, nt], F32, name="var", tag="var", bufs=2)
+            nc.gpsimd.tensor_scalar(
+                out=var[:], in0=state["total", gi][:], scalar1=1.0 / D, scalar2=EPS, op0=ALU.mult, op1=ALU.add
+            )
             rstd = work.tile([P, nt], F32, name="rstd", tag="rstd", bufs=3)
-            nc.vector.reciprocal(out=rstd[:], in_=state["root", gi][:])
+            nc.gpsimd.tensor_tensor(out=rstd[:], in0=var[:], in1=minus_half[:, 0:nt], op=ALU.pow)
             state["rstd", gi] = rstd
 
-        def unit_transpose(gi, t, hq):
-            bank = psum.tile([P, QUAD, HD], F32, name="wbank", tag="tbank", bufs=T_BANKS)
+        def unit_transpose(gi, t, hq, spare=False):
+            if spare:
+                bank = psum.tile([P, QUAD, HD], F32, name="obank", tag="acc", bufs=MX_BANKS)
+            else:
+                bank = psum.tile([P, QUAD, HD], F32, name="obank", tag="tbank", bufs=T_BANKS)
             for i in range(QUAD):
-                w = state["w", gi, hq * QUAD + i]
-                nc.tensor.transpose(bank[:, i, :], w[:, t * P : (t + 1) * P], ident[:])
+                h = hq * QUAD + i
+                ts = slice(t * P, (t + 1) * P)
+                nc.tensor.matmul(
+                    out=bank[:, i, :], lhsT=state["cosT", gi, h][:, ts], rhs=ident[:], start=True, stop=False, is_transpose=True
+                )
+                nc.tensor.matmul(
+                    out=bank[:, i, :], lhsT=state["sinT", gi, h][:, ts], rhs=swap[:], start=False, stop=True, is_transpose=True
+                )
             return bank
 
-        def store(gi, t, cs):
-            proj, chunk, t0 = GROUPS[gi][:3]
-            nc.sync.dma_start(out=outs[proj][(t0 + t) * P : (t0 + t + 1) * P, cs], in_=state["y", gi, t][:, cs])
-
-        def unit_rotate(gi, t, hq, bank):
-            proj, chunk, t0, nt, fold, late = GROUPS[gi]
-            if ("y", gi, t) not in state:
-                state["y", gi, t] = work.tile([P, D], F32, name="y", tag="y", bufs=T1_BUFS)
-                state["done", gi, t] = 0
-            y = state["y", gi, t]
-            t2 = work.tile([P, QUAD * HD], F32, name="t2", tag="t2", bufs=T2_BUFS)
-            cs = slice(hq * QUAD * HD, (hq + 1) * QUAD * HD)
-            pairs = bank[:].rearrange("p h (c e) -> p h c e", e=2)
-            shape = [P, QUAD, HD // 2, 2]
-            ctab = cos2[:, t0 + t : t0 + t + 1, :, :].to_broadcast(shape)
-            stab = sin2[:, t0 + t : t0 + t + 1, :, :].to_broadcast(shape)
-            o1 = y[:, cs].rearrange("p (h c e) -> p h c e", h=QUAD, e=2)
-            o2 = t2[:].rearrange("p (h c e) -> p h c e", h=QUAD, e=2)
-            if late:
-                nc.vector.tensor_tensor(out=o1, in0=pairs, in1=ctab, op=ALU.mult)
-                nc.vector.tensor_tensor(out=o2, in0=pairs[:, :, :, ::-1], in1=stab, op=ALU.mult)
+        def unit_finish(gi, t, hq, bank, on_vector):
+            proj, t0, nt = GROUPS[gi][:3]
+            y = work.tile([P, QUAD * HD], F32, name="y", tag="y", bufs=Y_BUFS)
+            r = state["rstd", gi][:, t : t + 1]
+            src = bank[:].rearrange("p h d -> p (h d)")
+            if on_vector:
+                nc.vector.tensor_scalar(out=y[:], in0=src, scalar1=r, scalar2=None, op0=ALU.mult)
             else:
-                r = state["rstd", gi][:, t : t + 1]
-                nc.vector.scalar_tensor_tensor(out=o1, in0=pairs, scalar=r, in1=ctab, op0=ALU.mult, op1=ALU.mult)
-                nc.vector.scalar_tensor_tensor(
-                    out=o2, in0=pairs[:, :, :, ::-1], scalar=r, in1=stab, op0=ALU.mult, op1=ALU.mult
-                )
-            state["count"] = state.get("count", 0) + 1
-            on_vector = state["count"] > NT * 2 * NH // QUAD - V_ADD_UNITS or state["count"] % V_ADD_EVERY == 0
-            adder = nc.vector if on_vector else nc.gpsimd
-            state["adds"].append((adder, y[:, cs], t2))
-            state["done", gi, t] += 1
-            complete = state["done", gi, t] == NH // QUAD
-            if late:
-                if complete:
-                    state["scale"].append((gi, t, state["si"] + SCALE_DELAY))
-            elif gi >= len(GROUPS) - TAIL_GROUPS:
-                state["stores"].append((gi, t, cs))
-            elif complete:
-                state["stores"].append((gi, t, slice(0, D)))
+                nc.scalar.activation(out=y[:], in_=src, func=ACT.Copy, scale=r)
+            nc.sync.dma_start(
+                out=outs[proj][(t0 + t) * P : (t0 + t + 1) * P, hq * QUAD * HD : (hq + 1) * QUAD * HD], in_=y[:]
+            )
 
-        def flush_adds():
-            for adder, ycs, t2 in state["adds"]:
-                adder.tensor_tensor(out=ycs, in0=ycs, in1=t2[:], op=ALU.add)
-            state["adds"] = []
-            for e in state["stores"]:
-                store(*e)
-            state["stores"] = []
-
-        def late_scale(entries):
-            for gi, t, due in entries:
-                y = state["y", gi, t]
-                r = state["rstd", gi][:, t : t + 1]
-                split = LATE_SPLIT if gi < len(GROUPS) - TAIL_GROUPS else TAIL_SPLIT
-                nc.scalar.activation(out=y[:, :split], in_=y[:, :split], func=ACT.Copy, scale=r)
-                if split < D:
-                    if gi < len(GROUPS) - TAIL_GROUPS:
-                        nc.gpsimd.tensor_scalar(out=y[:, split:], in0=y[:, split:], scalar1=r, scalar2=0.0, op0=ALU.mult, op1=ALU.add)
-                    else:
-                        nc.vector.tensor_scalar(out=y[:, split:], in0=y[:, split:], scalar1=r, scalar2=None, op0=ALU.mult)
-                if gi < len(GROUPS) - TAIL_GROUPS:
-                    store(gi, t, slice(0, D))
-                else:
-                    store(gi, t, slice(split, D))
-                    store(gi, t, slice(0, split))
-
-        state["adds"], state["stores"], state["scale"] = [], [], []
         steps = []
         for gi in range(len(GROUPS)):
-            jobs = NH * GROUPS[gi][3] // QUAD
+            jobs = NH * GROUPS[gi][2] // QUAD
             steps.extend((gi, list(range(j, min(j + STEP, jobs)))) for j in range(0, jobs, STEP))
         units = []
-        sq_ready = []
-        folding = {}
-        for si in range(len(steps) + 1):
+        closing = {}
+        parts = {}
+        prev_w = []
+        pending = []
+        count = 0
+        si = 0
+        while si < len(steps) or units or any(s >= si for s in closing) or prev_w:
             live = si < len(steps)
-            state["si"] = si
             accs = []
             if live:
                 gi, jobs = steps[si]
                 for job in jobs:
                     accs.append((job, mx_job(gi, job)))
             if si == 0:
-                params()
-            closing = []
-            for cgi, sq, first_one, last_one, due in sq_ready:
-                if due <= si:
-                    ss_transpose(cgi, sq, first_one, last_one)
-                    if last_one:
-                        closing.append(cgi)
-            sq_ready = [e for e in sq_ready if e[4] > si]
+                tables()
+            if si == K_PARAMS - 1:
+                widen_rows(1)
+            if si == K_PARAMS:
+                params(1)
+            if prev_w and ("cosT", GROUPS[prev_w[0][0]][1] // 4) not in state:
+                table_transpose(GROUPS[prev_w[0][0]][1] // 4)
             xs = []
             if live and later and si >= X_START:
                 for it in later[:X_PER_STEP]:
                     xs.append((it, x_transpose(*it)))
                 later = later[X_PER_STEP:]
-            take = min(UNITS_PER_STEP + (1 if len(units) > BACKLOG else 0), T_BANKS - len(xs))
-            now = units[:take]
-            units = units[take:]
-            banks = [unit_transpose(*u) for u in now]
-            for cgi in closing:
-                ss_reduce(cgi)
+            cgi = closing.get(si)
+            ready = [u for u in units if u[3] <= si]
+            take = min(UNITS_PER_STEP if live else TAIL_TAKE, (T_BANKS if si <= len(steps) else 4) - len(xs) - (cgi is not None))
+            now = ready[:take]
+            units = [u for u in units if u not in now]
+            banks = [unit_transpose(*u[:3], spare=(si > len(steps) and i % 2 == 1)) for i, u in enumerate(now)]
+            if cgi is not None:
+                ss_transpose(cgi, parts[cgi])
+            for pgi, job, w in prev_w:
+                rotate_job(pgi, job, w)
+            prev_w = []
             new_sq = []
             for i, (job, acc) in enumerate(accs):
-                new_sq.append((job, drain_job(gi, job, acc)))
-                if i == min(SQRT_AT, len(accs) - 1):
-                    for cgi in closing:
-                        ss_sqrt(cgi)
-            if not accs:
-                for cgi in closing:
-                    ss_sqrt(cgi)
-            ready = [e for e in state["scale"] if e[2] <= si and state.get(("rstd_step", e[0]), si) < si][:SCALES_PER_STEP]
-            late_scale(ready)
-            state["scale"] = [e for e in state["scale"] if e not in ready]
-            if si == 0:
-                tables()
-            for it, bank in xs:
-                x_copy(it[0], it[1], it[2], bank, on_scalar=X_ON_SCALAR)
+                w, sq = drain_job(gi, job, acc)
+                prev_w.append((gi, job, w))
+                new_sq.append((job, sq))
+            for i, (it, bank) in enumerate(xs):
+                x_copy(it[0], it[1], it[2], bank, on_scalar=i < X_ON_SCALAR)
             for u, bank in zip(now, banks):
-                unit_rotate(u[0], u[1], u[2], bank)
-            flush_adds()
+                count += 1
+                unit_finish(u[0], u[1], u[2], bank, on_vector=(count % V_EVERY < V_NUM) if live else (count % 2 == 0))
+            if cgi is not None:
+                ss_reduce(cgi)
+                units.extend(
+                    (cgi, t, hq, si + UNIT_DELAY) for hq in range(NH // QUAD) for t in range(GROUPS[cgi][2])
+                )
             for it, bank in xs:
                 if it[2] + 2 >= CHUNKS[it[0]][1]:
                     x_quantize(it[0], it[1])
-            for cgi in closing:
-                ss_recip(cgi)
-                state["rstd_step", cgi] = si
-                if not GROUPS[cgi][5]:
-                    units.extend((cgi, t, hq) for t in range(GROUPS[cgi][3]) for hq in range(NH // QUAD))
             for job, sq in new_sq:
-                nt, fold, late = GROUPS[gi][3:6]
+                nt, unfolded = GROUPS[gi][2:4]
                 njobs = NH * nt // QUAD
-                if job % fold == 0:
-                    folding[gi] = sq
-                else:
+                if job == 0:
+                    parts[gi] = [sq]
+                elif job < njobs - unfolded:
                     acc_sq = work.tile([P, QUAD * P], F32, name="sqsum", tag="sqsum", bufs=3)
-                    nc.vector.tensor_tensor(out=acc_sq[:], in0=folding[gi][:], in1=sq[:], op=ALU.add)
-                    folding[gi] = acc_sq
-                if job % fold == fold - 1 or job == njobs - 1:
-                    sq_ready.append((gi, folding[gi], job < fold, job == njobs - 1, si + (2 if fold > 1 else 1)))
-                if late and (job + 1) % nt == 0:
-                    units.extend((gi, t, job // nt) for t in range(nt))
-        while units:
-            now = units[:2]
-            units = units[2:]
-            banks = [unit_transpose(*u) for u in now]
-            for u, bank in zip(now, banks):
-                unit_rotate(u[0], u[1], u[2], bank)
-                flush_adds()
-        late_scale(state["scale"])
+                    nc.gpsimd.tensor_tensor(out=acc_sq[:], in0=parts[gi][0][:], in1=sq[:], op=ALU.add)
+                    parts[gi][0] = acc_sq
+                else:
+                    parts[gi].append(sq)
+                if job == njobs - 1:
+                    closing[si + GROUPS[gi][4]] = gi
+            if cgi is not None:
+                ss_rstd(cgi)
+            si += 1

@@ -24,24 +24,37 @@ QUAD = 4
 NT = L // P
 
 CHUNKS = [(0, 2), (2, 2), (4, 4)]
-GROUPS = [(0, 0, 2, 0, 2), (0, 2, 2, 0, 2), (1, 0, 4, 0, 2), (0, 4, 4, 0, 2), (1, 4, 4, 2, 1)]
+GROUPS = [(0, 0, 2, 1, 1), (0, 2, 2, 1, 1), (0, 4, 4, 1, 1), (1, 4, 4, 1, 1)]
 K_BEFORE = 2
 STEP = 2
 T_BANKS = 3
 MX_BANKS = 3
-SQ_BUFS = 8
+SQ_BUFS = 3
 W_BUFS = 5
-PROD_BUFS = 42
-Y_BUFS = 8
+PROD_BUFS = 34
+Y_BUFS = 5
 UNITS_PER_STEP = 2
 X_START = 0
 X_PER_STEP = 2
 X_ON_SCALAR = 1
-V_EVERY = 2
-UNIT_DELAY = 2
+V_EVERY = 4
+UNIT_DELAY = 1
 V_NUM = 1
 TAIL_TAKE = 4
-K_PARAMS = 4
+K_PARAMS = 8
+K_AFTER = 2
+A_TILES = 4
+A_START = 5
+A_SPAN = 9
+A_DELAY = 2
+A_POOL_TAIL = 1
+TAIL_V = 2
+A_STORE_DELAY = 1
+CATCH_UP = 100
+A_EARLY = 2
+A_LATE_AT = -1
+A_V_GAINS = 3
+A_V_ADDS = 1
 
 
 def tile_causalwanselfattention_pa_kernel(
@@ -122,12 +135,17 @@ def tile_causalwanselfattention_pa_kernel(
         nc.sync.dma_start(out=sin_in[:], in_=freqs_sin.rearrange("(t p) c -> p t c", p=P))
         load_w(0, 4, NH)
         for chunk in range(1, len(CHUNKS)):
-            if chunk == K_BEFORE:
-                load_scales(1)
-                load_w(1, 0, NH)
-                load_rows(nc.sync, 1)
             for g in range(PASSES):
                 load_x(chunk, g)
+            if chunk == K_AFTER:
+                load_scales(1)
+                load_w(1, 0, NH)
+        load_rows(nc.sync, 1)
+        bk_all = keep.tile([P, D], BF16, name="bk_all")
+        gk_all = keep.tile([P, D], BF16, name="gk_all")
+        if A_TILES:
+            nc.sync.dma_start(out=bk_all[:], in_=bk.partition_broadcast(P))
+            nc.sync.dma_start(out=gk_all[:], in_=gk.partition_broadcast(P))
 
         xcodes, xscales, grouped = {}, {}, {}
         for half in range(2):
@@ -149,7 +167,7 @@ def tile_causalwanselfattention_pa_kernel(
             nt = CHUNKS[chunk][1]
             nj = min(2, nt - j0)
             if j0 == 0:
-                grouped[chunk, g] = work.tile([P, nt * P * 4], BF16, name="grouped", tag="grouped", bufs=3, align_bytes=64)
+                grouped[chunk, g] = work.tile([P, nt * P * 4], BF16, name="grouped", tag="grouped", bufs=2, align_bytes=64)
             dst = grouped[chunk, g][:].bitcast(F32)[:, j0 * 256 : (j0 + nj) * 256].rearrange("p (j r u) -> p j r u", j=nj, u=2)
             src = bank[:].rearrange("p j u r -> p j r u")
             if on_scalar:
@@ -180,15 +198,17 @@ def tile_causalwanselfattention_pa_kernel(
             nc.vector.tensor_copy(out=cols[proj][:], in_=pbank[:, 0 : 2 * NH])
             nc.vector.tensor_tensor(out=gb[proj][:], in0=cols[proj][:, 0:NH], in1=cols[proj][:, NH : 2 * NH], op=ALU.mult)
 
-        cos2 = keep.tile([P, NT, HD // 2, 2], F32, name="cos2")
-        sin2 = keep.tile([P, NT, HD // 2, 2], F32, name="sin2")
+        cos2 = keep.tile([P, NT, HD // 2, 2], BF16, name="cos2")
+        sin2 = keep.tile([P, NT, HD // 2, 2], BF16, name="sin2")
         swap = keep.tile([P, P], F32, name="swap")
+        ident16 = keep.tile([P, P], BF16, name="ident16")
 
         def tables():
             shape = [P, NT * HD // 2, 2]
             nc.vector.tensor_copy(
                 out=swap[:].rearrange("p (c e) -> p c e", e=2), in_=ident[:].rearrange("p (c e) -> p c e", e=2)[:, :, ::-1]
             )
+            nc.vector.tensor_copy(out=ident16[:], in_=ident[:])
             sign = keep.tile([P, 1, 2], F32, name="sign")
             nc.vector.memset(sign[:, :, 0:1], 1.0)
             nc.vector.memset(sign[:, :, 1:2], -1.0)
@@ -221,11 +241,83 @@ def tile_causalwanselfattention_pa_kernel(
             return range(job * hb, (job + 1) * hb)
 
         def table_transpose(half):
-            for name, src in (("cosT", cos2), ("sinT", sin2)):
-                bank = psum.tile([P, 4, P], F32, name=name, tag=name, bufs=1)
+            bank = psum.tile([P, 2, 4, P], BF16, name="tabT", tag="tabT", bufs=1)
+            for i, (name, src) in enumerate((("cosT", cos2), ("sinT", sin2))):
                 for t in range(4):
-                    nc.tensor.transpose(bank[:, t, :], src[:, half * 4 + t, :, :].rearrange("p c e -> p (c e)"), ident[:])
-                state[name, half] = bank
+                    nc.tensor.transpose(
+                        bank[:, i, t, :], src[:, half * 4 + t, :, :].rearrange("p c e -> p (c e)"), ident16[:]
+                    )
+                state[name, half] = bank[:, i, :, :]
+
+        def table_tokens():
+            bank = psum.tile([P, 2, 4 * P], BF16, name="tabA", tag="tabA", bufs=1)
+            for i, src in enumerate((cos2, sin2)):
+                nc.tensor.matmul(
+                    out=bank[:, i, :], lhsT=ident16[:], rhs=src[:, 0:4, :, :].rearrange("p t c e -> p (t c e)"),
+                    start=True, stop=True,
+                )
+            state["tabA"] = bank
+
+        def a_matmul(t, j):
+            acc = psum.tile([P, 512], F32, name="acc", tag="acc", bufs=MX_BANKS)
+            wt = wcodes[1, 0][0]
+            for g in range(PASSES):
+                nc.tensor.matmul_mx(
+                    out=acc[:],
+                    lhsT=xcodes[0, g][:, t * P : (t + 1) * P].bitcast(FP8X4),
+                    lhsT_scale=xscales[0, g][:, t * P : (t + 1) * P],
+                    rhs=wt[:, g, j * 1024 : (j + 1) * 1024].bitcast(FP4X4),
+                    rhs_scale=planes[1][:, g, j * 512 : (j + 1) * 512],
+                    start=(g == 0),
+                    stop=(g == PASSES - 1),
+                )
+            return acc
+
+        def a_bias(t, j, acc):
+            if j == 0:
+                state["u", t] = work.tile([P, D], F32, name="u", tag="u", bufs=2)
+                state["aw", t] = work.tile([P, D], F32, name="aw", tag="aw", bufs=2)
+                state["part", t] = work.tile([P, 3], F32, name="part", tag="part", bufs=2)
+            cs = slice(j * 512, (j + 1) * 512)
+            nc.vector.tensor_tensor(out=state["u", t][:, cs], in0=acc[:], in1=bk_all[:, cs], op=ALU.add)
+
+        def a_square(t, j):
+            cs = slice(j * 512, (j + 1) * 512)
+            junk = work.tile([P, 512], BF16, name="junk", tag="junk", bufs=1)
+            nc.scalar.activation(
+                out=junk[:], in_=state["u", t][:, cs], func=ACT.Square, accum_out=state["part", t][:, j : j + 1]
+            )
+
+        def a_gain(t, j, eng):
+            cs = slice(j * 512, (j + 1) * 512)
+            eng.tensor_tensor(out=state["aw", t][:, cs], in0=state["u", t][:, cs], in1=gk_all[:, cs], op=ALU.mult)
+
+        def a_total(t):
+            total = work.tile([P, 1], F32, name="atotal", tag="atotal", bufs=2)
+            nc.vector.tensor_reduce(out=total[:], in_=state["part", t][:], axis=AXIS.X, op=ALU.add)
+            state["total", "a", t] = total
+
+        def a_products(t, j):
+            cs = slice(j * 512, (j + 1) * 512)
+            shape = [P, QUAD, HD // 2, 2]
+            pairs = state["aw", t][:, cs].rearrange("p (h c e) -> p h c e", h=QUAD, e=2)
+            r = state["rstd", "a", t][:, 0:1]
+            res = []
+            for i, src in enumerate((pairs[:, :, :, ::-1], pairs)):
+                tab = state["tabA"][:, 1 - i, t * P : (t + 1) * P].rearrange("p (o c e) -> p o c e", o=1, e=2)
+                prod = work.tile([P, 512], F32, name="aprod", tag="aprod%d" % i, bufs=2 + 2 * i)
+                nc.vector.scalar_tensor_tensor(
+                    out=prod[:].rearrange("p (h c e) -> p h c e", h=QUAD, e=2), in0=src, scalar=r,
+                    in1=tab.to_broadcast(shape), op0=ALU.mult, op1=ALU.mult,
+                )
+                res.append(prod)
+            return res
+
+        def a_finish(t, j, res, adder):
+            adder.tensor_tensor(out=res[1][:], in0=res[1][:], in1=res[0][:], op=ALU.subtract)
+
+        def a_store(t, j, res):
+            nc.sync.dma_start(out=outs[1][t * P : (t + 1) * P, j * 512 : (j + 1) * 512], in_=res[1][:])
 
         def mx_job(gi, job):
             proj, t0, nt = GROUPS[gi][:3]
@@ -245,9 +337,8 @@ def tile_causalwanselfattention_pa_kernel(
                     )
             return acc
 
-        def drain_job(gi, job, acc):
+        def drain_job(gi, job, acc, sq):
             proj, t0, nt = GROUPS[gi][:3]
-            sq = work.tile([P, QUAD * P], F32, name="sq", tag="sq", bufs=SQ_BUFS)
             w = work.tile([P, QUAD * P], F32, name="w", tag="w", bufs=W_BUFS)
             n = nt * P
             for i, h in enumerate(job_heads(gi, job)):
@@ -259,7 +350,7 @@ def tile_causalwanselfattention_pa_kernel(
                 nc.scalar.activation(
                     out=sq[:, i * n : (i + 1) * n], in_=acc[:, i, :], func=ACT.Square, bias=cols[proj][:, h : h + 1]
                 )
-            return w, sq
+            return w
 
         def rotate_job(gi, job, w):
             proj, t0, nt = GROUPS[gi][:3]
@@ -277,7 +368,7 @@ def tile_causalwanselfattention_pa_kernel(
             nt = GROUPS[gi][2]
             bank = psum.tile([P, nt, P], F32, name="ss", tag="tbank", bufs=T_BANKS)
             for t in range(nt):
-                blocks = [sq[:, b * P : (b + 1) * P] for sq in parts for b in range(t, QUAD, nt)]
+                blocks = [sq[:, b * P : (b + 1) * P] for sq in parts for b in range(t, sq.shape[1] // P, nt)]
                 for i, blk in enumerate(blocks):
                     nc.tensor.matmul(
                         out=bank[:, t, :], lhsT=blk, rhs=ident[:],
@@ -291,15 +382,14 @@ def tile_causalwanselfattention_pa_kernel(
             nc.vector.tensor_reduce(out=total[:], in_=state["ss", gi][:], axis=AXIS.X, op=ALU.add)
             state["total", gi] = total
 
-        def ss_rstd(gi):
-            nt = GROUPS[gi][2]
+        def ss_rstd(key, nt):
             var = work.tile([P, nt], F32, name="var", tag="var", bufs=2)
             nc.gpsimd.tensor_scalar(
-                out=var[:], in0=state["total", gi][:], scalar1=1.0 / D, scalar2=EPS, op0=ALU.mult, op1=ALU.add
+                out=var[:], in0=state[("total",) + key][:], scalar1=1.0 / D, scalar2=EPS, op0=ALU.mult, op1=ALU.add
             )
-            rstd = work.tile([P, nt], F32, name="rstd", tag="rstd", bufs=3)
+            rstd = work.tile([P, nt], F32, name="rstd", tag="rstd", bufs=4)
             nc.gpsimd.tensor_tensor(out=rstd[:], in0=var[:], in1=minus_half[:, 0:nt], op=ALU.pow)
-            state["rstd", gi] = rstd
+            state[("rstd",) + key] = rstd
 
         def unit_transpose(gi, t, hq, spare=False):
             if spare:
@@ -334,22 +424,33 @@ def tile_causalwanselfattention_pa_kernel(
         for gi in range(len(GROUPS)):
             jobs = NH * GROUPS[gi][2] // QUAD
             steps.extend((gi, list(range(j, min(j + STEP, jobs)))) for j in range(0, jobs, STEP))
+        a_units = [(t, j) for t in range(A_TILES) for j in range(3)]
+        early = a_units[: 3 * A_EARLY]
+        a_at = {A_START + (i * A_SPAN) // len(early): u for i, u in enumerate(early)}
+        a_at.update({len(steps) + A_LATE_AT + i: u for i, u in enumerate(a_units[3 * A_EARLY :])})
+        last_mx = max(list(a_at) + [len(steps) - 1])
+        a_prod_at = {}
+        a_stores = []
         units = []
         closing = {}
         parts = {}
         prev_w = []
-        pending = []
         count = 0
         si = 0
-        while si < len(steps) or units or any(s >= si for s in closing) or prev_w:
+        while si <= last_mx or units or any(s >= si for s in closing) or prev_w or any(s + A_STORE_DELAY >= si for s in a_prod_at):
             live = si < len(steps)
             accs = []
+            a_now = a_at.get(si)
+            if a_now is not None:
+                a_acc = a_matmul(*a_now)
             if live:
                 gi, jobs = steps[si]
                 for job in jobs:
                     accs.append((job, mx_job(gi, job)))
             if si == 0:
                 tables()
+            if si == A_START and A_TILES:
+                table_tokens()
             if si == K_PARAMS - 1:
                 widen_rows(1)
             if si == K_PARAMS:
@@ -363,46 +464,70 @@ def tile_causalwanselfattention_pa_kernel(
                 later = later[X_PER_STEP:]
             cgi = closing.get(si)
             ready = [u for u in units if u[3] <= si]
-            take = min(UNITS_PER_STEP if live else TAIL_TAKE, (T_BANKS if si <= len(steps) else 4) - len(xs) - (cgi is not None))
+            take = min(UNITS_PER_STEP + (si >= CATCH_UP) if si <= last_mx else TAIL_TAKE, (T_BANKS if si <= last_mx + 1 else 4) - len(xs) - (cgi is not None))
             now = ready[:take]
             units = [u for u in units if u not in now]
-            banks = [unit_transpose(*u[:3], spare=(si > len(steps) and i % 2 == 1)) for i, u in enumerate(now)]
+            banks = [unit_transpose(*u[:3], spare=(si > last_mx + 1 and i % 2 == 1)) for i, u in enumerate(now)]
             if cgi is not None:
                 ss_transpose(cgi, parts[cgi])
+            if a_now is not None:
+                a_bias(a_now[0], a_now[1], a_acc)
             for pgi, job, w in prev_w:
                 rotate_job(pgi, job, w)
             prev_w = []
-            new_sq = []
+            a_res = [(u, a_products(*u)) for u in a_prod_at.get(si, [])]
+            if live:
+                sq = work.tile([P, len(accs) * QUAD * P], F32, name="sq", tag="sq", bufs=SQ_BUFS)
             for i, (job, acc) in enumerate(accs):
-                w, sq = drain_job(gi, job, acc)
+                w = drain_job(gi, job, acc, sq[:, i * QUAD * P : (i + 1) * QUAD * P])
                 prev_w.append((gi, job, w))
-                new_sq.append((job, sq))
+            if a_now is not None:
+                a_square(*a_now)
+                if 3 * a_now[0] + a_now[1] >= 3 * A_TILES - A_V_GAINS:
+                    a_gain(a_now[0], a_now[1], nc.vector)
+                elif a_now[1] < 2:
+                    a_gain(a_now[0], a_now[1], nc.gpsimd)
+            for u, res in a_res:
+                a_finish(u[0], u[1], res, nc.vector if 3 * u[0] + u[1] >= 3 * A_TILES - A_V_ADDS else nc.gpsimd)
+            a_stores.extend((si + A_STORE_DELAY, u, res) for u, res in a_res)
             for i, (it, bank) in enumerate(xs):
                 x_copy(it[0], it[1], it[2], bank, on_scalar=i < X_ON_SCALAR)
             for u, bank in zip(now, banks):
                 count += 1
-                unit_finish(u[0], u[1], u[2], bank, on_vector=(count % V_EVERY < V_NUM) if live else (count % 2 == 0))
+                unit_finish(u[0], u[1], u[2], bank, on_vector=(count % V_EVERY < V_NUM) if live else (count % TAIL_V == 0 and si > last_mx + 3))
+            for due, u, res in a_stores:
+                if due == si:
+                    a_store(u[0], u[1], res)
             if cgi is not None:
                 ss_reduce(cgi)
                 units.extend(
                     (cgi, t, hq, si + UNIT_DELAY) for hq in range(NH // QUAD) for t in range(GROUPS[cgi][2])
                 )
+            if a_now is not None and a_now[1] == 2:
+                a_total(a_now[0])
+                for j in range(3):
+                    a_prod_at.setdefault(si + (A_DELAY + (j * A_SPAN) // len(early) if a_now[0] < A_EARLY else 1 + j), []).append((a_now[0], j))
             for it, bank in xs:
                 if it[2] + 2 >= CHUNKS[it[0]][1]:
                     x_quantize(it[0], it[1])
-            for job, sq in new_sq:
+            if live:
                 nt, unfolded = GROUPS[gi][2:4]
                 njobs = NH * nt // QUAD
-                if job == 0:
+                if jobs[0] == 0:
                     parts[gi] = [sq]
-                elif job < njobs - unfolded:
-                    acc_sq = work.tile([P, QUAD * P], F32, name="sqsum", tag="sqsum", bufs=3)
+                elif jobs[0] < njobs - unfolded * STEP:
+                    acc_sq = work.tile([P, STEP * QUAD * P], F32, name="sqsum", tag="sqsum", bufs=2)
                     nc.gpsimd.tensor_tensor(out=acc_sq[:], in0=parts[gi][0][:], in1=sq[:], op=ALU.add)
                     parts[gi][0] = acc_sq
                 else:
                     parts[gi].append(sq)
-                if job == njobs - 1:
+                if jobs[-1] == njobs - 1:
+                    assert si + GROUPS[gi][4] not in closing
                     closing[si + GROUPS[gi][4]] = gi
             if cgi is not None:
-                ss_rstd(cgi)
+                ss_rstd((cgi,), GROUPS[cgi][2])
+            if a_now is not None and a_now[1] == 2:
+                ss_rstd(("a", a_now[0]), 1)
+                if 3 * a_now[0] + a_now[1] < 3 * A_TILES - A_V_GAINS:
+                    a_gain(a_now[0], a_now[1], nc.gpsimd)
             si += 1

from contextlib import ExitStack

import concourse.mybir as mybir
from concourse.masks import make_identity

L, D, NH, HD = 1024, 1536, 12, 128
EPS = 1e-6
FLOPS = 2 * 2 * L * D * D

F32 = mybir.dt.float32
BF16 = mybir.dt.bfloat16
I32 = mybir.dt.int32
U32 = mybir.dt.uint32
U8 = mybir.dt.uint8
FP8X4 = mybir.dt.float8_e5m2_x4
FP4X4 = mybir.dt.float4_e2m1fn_x4
ALU = mybir.AluOpType
ACT = mybir.ActivationFunctionType
AXIS = mybir.AxisListType

P = 128
PASSES = D // 512
QUAD = 4
NT = L // P

CHUNKS = [(0, 2), (2, 2), (4, 4)]
GROUPS = [(0, 0, 2, 1, 1), (0, 2, 2, 1, 1), (0, 4, 4, 1, 1), (1, 4, 4, 1, 1)]
K_BEFORE = 2
STEP = 2
T_BANKS = 3
MX_BANKS = 3
SQ_BUFS = 3
W_BUFS = 5
PROD_BUFS = 34
Y_BUFS = 5
UNITS_PER_STEP = 2
X_START = 0
X_PER_STEP = 2
X_ON_SCALAR = 1
V_EVERY = 4
UNIT_DELAY = 1
V_NUM = 1
TAIL_TAKE = 4
K_PARAMS = 8
K_AFTER = 2
A_TILES = 4
A_START = 5
A_SPAN = 9
A_DELAY = 2
A_POOL_TAIL = 1
TAIL_V = 2
A_STORE_DELAY = 1
CATCH_UP = 100
A_EARLY = 2
A_LATE_AT = -1
A_V_GAINS = 3
A_V_ADDS = 1


def tile_causalwanselfattention_pa_kernel(
    tc, x, wq_words, wq_scales, wk_words, wk_scales, bq, bk, gq, gk, freqs_cos, freqs_sin, out_0, out_1
):
    nc = tc.nc
    x2 = x.rearrange("b l d -> (b l) d")
    outs = [o.rearrange("b l h d -> (b l) (h d)") for o in (out_0, out_1)]
    words_in = (wq_words, wk_words)
    scales_in = (wq_scales, wk_scales)

    with ExitStack() as ctx:
        keep = ctx.enter_context(tc.tile_pool(name="keep", bufs=1))
        work = ctx.enter_context(tc.tile_pool(name="work", bufs=1))
        psum = ctx.enter_context(tc.psum_pool(name="psum", bufs=1))
        ctx.enter_context(tc.manual_schedule())

        ident = keep.tile([P, P], F32, name="ident")
        make_identity(nc, ident[:])

        planes = []
        for proj in range(2):
            plane = keep.tile([P, PASSES, D], U8, name="wplane%d" % proj, align_bytes=64)
            planes.append(plane)
        rows32 = [keep.tile([P, P], F32, name="rows32_%d" % proj) for proj in range(2)]
        minus_half = keep.tile([P, 4], F32, name="minus_half")
        nc.vector.memset(planes[0][:].rearrange("p g n -> p (g n)").bitcast(I32), 0)
        nc.vector.memset(rows32[0][:], 0.0)
        nc.vector.memset(planes[1][:].rearrange("p g n -> p (g n)").bitcast(I32), 0)
        nc.vector.memset(rows32[1][:], 0.0)
        nc.vector.memset(minus_half[:], -0.5)

        xraw = {}

        def load_x(chunk, g):
            t0, nt = CHUNKS[chunk]
            t = keep.tile([P, nt, 512], BF16, name="xraw%d_%d" % (chunk, g))
            nc.sync.dma_start(
                out=t[:],
                in_=x2[t0 * P : (t0 + nt) * P, g * 512 : (g + 1) * 512].rearrange("(t p) k -> p t k", p=P),
            )
            xraw[chunk, g] = t

        def load_scales(proj):
            for q in range(4):
                nc.sync.dma_start(
                    out=planes[proj][32 * q : 32 * q + 4, :, :].bitcast(I32),
                    in_=scales_in[proj][:, 4 * q : 4 * q + 4, :].rearrange("g r n -> r g n").bitcast(I32),
                )

        wcodes = {}

        def load_w(proj, h0, h1):
            t = keep.tile([P, PASSES, (h1 - h0) * 2 * HD], U8, name="w%d_%d" % (proj, h0), align_bytes=64)
            nc.sync.dma_start(
                out=t[:].bitcast(I32),
                in_=words_in[proj][:, :, h0 * 2 * HD : h1 * 2 * HD].rearrange("g p n -> p g n").bitcast(I32),
            )
            for h in range(h0, h1):
                wcodes[proj, h] = (t, h - h0)

        rows16 = [keep.tile([2 * NH, HD], BF16, name="rows16_%d" % proj) for proj in range(2)]

        def load_rows(queue, proj):
            for i, vec in enumerate(((bq, gq), (bk, gk))[proj]):
                queue.dma_start(out=rows16[proj][i * NH : (i + 1) * NH, :], in_=vec.rearrange("(h d) -> h d", d=HD))

        load_rows(nc.scalar, 0)

        cos_in = keep.tile([P, NT, HD // 2], BF16, name="cos_in")
        sin_in = keep.tile([P, NT, HD // 2], BF16, name="sin_in")

        for g in range(PASSES):
            load_x(0, g)
        load_scales(0)
        load_w(0, 0, 4)
        nc.sync.dma_start(out=cos_in[:], in_=freqs_cos.rearrange("(t p) c -> p t c", p=P))
        nc.sync.dma_start(out=sin_in[:], in_=freqs_sin.rearrange("(t p) c -> p t c", p=P))
        load_w(0, 4, NH)
        for chunk in range(1, len(CHUNKS)):
            for g in range(PASSES):
                load_x(chunk, g)
            if chunk == K_AFTER:
                load_scales(1)
                load_w(1, 0, NH)
        load_rows(nc.sync, 1)
        bk_all = keep.tile([P, D], BF16, name="bk_all")
        gk_all = keep.tile([P, D], BF16, name="gk_all")
        if A_TILES:
            nc.sync.dma_start(out=bk_all[:], in_=bk.partition_broadcast(P))
            nc.sync.dma_start(out=gk_all[:], in_=gk.partition_broadcast(P))

        xcodes, xscales, grouped = {}, {}, {}
        for half in range(2):
            for g in range(PASSES):
                xcodes[half, g] = keep.tile([P, 512], U32, name="xc%d_%d" % (half, g), align_bytes=64)
                xscales[half, g] = keep.tile([P, 512], U8, name="xs%d_%d" % (half, g), align_bytes=64)

        def x_transpose(chunk, g, j0):
            nt = CHUNKS[chunk][1]
            nj = min(2, nt - j0)
            bank = psum.tile([P, nj, 2, P], F32, name="xbank", tag="tbank", bufs=T_BANKS)
            words = xraw[chunk, g][:].bitcast(F32)
            for j in range(nj):
                for u in range(2):
                    nc.tensor.transpose(bank[:, j, u, :], words[:, j0 + j, u : 256 : 2], ident[:])
            return bank

        def x_copy(chunk, g, j0, bank, on_scalar):
            nt = CHUNKS[chunk][1]
            nj = min(2, nt - j0)
            if j0 == 0:
                grouped[chunk, g] = work.tile([P, nt * P * 4], BF16, name="grouped", tag="grouped", bufs=2, align_bytes=64)
            dst = grouped[chunk, g][:].bitcast(F32)[:, j0 * 256 : (j0 + nj) * 256].rearrange("p (j r u) -> p j r u", j=nj, u=2)
            src = bank[:].rearrange("p j u r -> p j r u")
            if on_scalar:
                nc.scalar.copy(out=dst, in_=src)
            else:
                nc.vector.tensor_copy(out=dst, in_=src)

        def x_quantize(chunk, g):
            t0, nt = CHUNKS[chunk]
            cs = slice(t0 % 4 * P, (t0 % 4 + nt) * P)
            nc.vector.quantize_mx(
                out=xcodes[t0 // 4, g][:, cs].bitcast(FP8X4), scales=xscales[t0 // 4, g][:, cs], in_=grouped[chunk, g][:]
            )

        x_items = [
            (chunk, g, j0) for chunk in range(len(CHUNKS)) for g in range(PASSES) for j0 in range(0, CHUNKS[chunk][1], 2)
        ]

        cols = [keep.tile([P, 2 * NH], F32, name="cols%d" % proj) for proj in range(2)]
        gb = [keep.tile([P, NH], F32, name="gb%d" % proj) for proj in range(2)]

        def widen_rows(proj):
            nc.vector.tensor_copy(out=rows32[proj][0 : 2 * NH, :], in_=rows16[proj][:])

        def params(proj):
            pbank = psum.tile([P, P], F32, name="pbank", tag="tbank", bufs=T_BANKS)
            nc.tensor.transpose(pbank[:], rows32[proj][:], ident[:])
            nc.vector.tensor_copy(out=cols[proj][:], in_=pbank[:, 0 : 2 * NH])
            nc.vector.tensor_tensor(out=gb[proj][:], in0=cols[proj][:, 0:NH], in1=cols[proj][:, NH : 2 * NH], op=ALU.mult)

        cos2 = keep.tile([P, NT, HD // 2, 2], BF16, name="cos2")
        sin2 = keep.tile([P, NT, HD // 2, 2], BF16, name="sin2")
        swap = keep.tile([P, P], F32, name="swap")
        ident16 = keep.tile([P, P], BF16, name="ident16")

        def tables():
            shape = [P, NT * HD // 2, 2]
            nc.vector.tensor_copy(
                out=swap[:].rearrange("p (c e) -> p c e", e=2), in_=ident[:].rearrange("p (c e) -> p c e", e=2)[:, :, ::-1]
            )
            nc.vector.tensor_copy(out=ident16[:], in_=ident[:])
            sign = keep.tile([P, 1, 2], F32, name="sign")
            nc.vector.memset(sign[:, :, 0:1], 1.0)
            nc.vector.memset(sign[:, :, 1:2], -1.0)
            nc.vector.tensor_copy(
                out=cos2[:].rearrange("p t c e -> p (t c) e"),
                in_=cos_in[:].rearrange("p t (c e) -> p (t c) e", e=1).to_broadcast(shape),
            )
            nc.vector.tensor_tensor(
                out=sin2[:].rearrange("p t c e -> p (t c) e"),
                in0=sin_in[:].rearrange("p t (c e) -> p (t c) e", e=1).to_broadcast(shape),
                in1=sign[:].to_broadcast(shape),
                op=ALU.mult,
            )

        first = [it for it in x_items if it[0] == 0]
        later = [it for it in x_items if it[0] != 0]
        widen_rows(0)
        for i, (chunk, g, j0) in enumerate(first):
            bank = x_transpose(chunk, g, j0)
            x_copy(chunk, g, j0, bank, on_scalar=(i % 2 == 1) or CHUNKS[0][1] <= 2)
            if i == len(first) - 1:
                params(0)
            if j0 + 2 >= CHUNKS[chunk][1]:
                x_quantize(chunk, g)

        state = {}

        def job_heads(gi, job):
            hb = QUAD // GROUPS[gi][2]
            return range(job * hb, (job + 1) * hb)

        def table_transpose(half):
            bank = psum.tile([P, 2, 4, P], BF16, name="tabT", tag="tabT", bufs=1)
            for i, (name, src) in enumerate((("cosT", cos2), ("sinT", sin2))):
                for t in range(4):
                    nc.tensor.transpose(
                        bank[:, i, t, :], src[:, half * 4 + t, :, :].rearrange("p c e -> p (c e)"), ident16[:]
                    )
                state[name, half] = bank[:, i, :, :]

        def table_tokens():
            bank = psum.tile([P, 2, 4 * P], BF16, name="tabA", tag="tabA", bufs=1)
            for i, src in enumerate((cos2, sin2)):
                nc.tensor.matmul(
                    out=bank[:, i, :], lhsT=ident16[:], rhs=src[:, 0:4, :, :].rearrange("p t c e -> p (t c e)"),
                    start=True, stop=True,
                )
            state["tabA"] = bank

        def a_matmul(t, j):
            acc = psum.tile([P, 512], F32, name="acc", tag="acc", bufs=MX_BANKS)
            wt = wcodes[1, 0][0]
            for g in range(PASSES):
                nc.tensor.matmul_mx(
                    out=acc[:],
                    lhsT=xcodes[0, g][:, t * P : (t + 1) * P].bitcast(FP8X4),
                    lhsT_scale=xscales[0, g][:, t * P : (t + 1) * P],
                    rhs=wt[:, g, j * 1024 : (j + 1) * 1024].bitcast(FP4X4),
                    rhs_scale=planes[1][:, g, j * 512 : (j + 1) * 512],
                    start=(g == 0),
                    stop=(g == PASSES - 1),
                )
            return acc

        def a_bias(t, j, acc):
            if j == 0:
                state["u", t] = work.tile([P, D], F32, name="u", tag="u", bufs=2)
                state["aw", t] = work.tile([P, D], F32, name="aw", tag="aw", bufs=2)
                state["part", t] = work.tile([P, 3], F32, name="part", tag="part", bufs=2)
            cs = slice(j * 512, (j + 1) * 512)
            nc.vector.tensor_tensor(out=state["u", t][:, cs], in0=acc[:], in1=bk_all[:, cs], op=ALU.add)

        def a_square(t, j):
            cs = slice(j * 512, (j + 1) * 512)
            junk = work.tile([P, 512], BF16, name="junk", tag="junk", bufs=1)
            nc.scalar.activation(
                out=junk[:], in_=state["u", t][:, cs], func=ACT.Square, accum_out=state["part", t][:, j : j + 1]
            )

        def a_gain(t, j, eng):
            cs = slice(j * 512, (j + 1) * 512)
            eng.tensor_tensor(out=state["aw", t][:, cs], in0=state["u", t][:, cs], in1=gk_all[:, cs], op=ALU.mult)

        def a_total(t):
            total = work.tile([P, 1], F32, name="atotal", tag="atotal", bufs=2)
            nc.vector.tensor_reduce(out=total[:], in_=state["part", t][:], axis=AXIS.X, op=ALU.add)
            state["total", "a", t] = total

        def a_products(t, j):
            cs = slice(j * 512, (j + 1) * 512)
            shape = [P, QUAD, HD // 2, 2]
            pairs = state["aw", t][:, cs].rearrange("p (h c e) -> p h c e", h=QUAD, e=2)
            r = state["rstd", "a", t][:, 0:1]
            res = []
            for i, src in enumerate((pairs[:, :, :, ::-1], pairs)):
                tab = state["tabA"][:, 1 - i, t * P : (t + 1) * P].rearrange("p (o c e) -> p o c e", o=1, e=2)
                prod = work.tile([P, 512], F32, name="aprod", tag="aprod%d" % i, bufs=2 + 2 * i)
                nc.vector.scalar_tensor_tensor(
                    out=prod[:].rearrange("p (h c e) -> p h c e", h=QUAD, e=2), in0=src, scalar=r,
                    in1=tab.to_broadcast(shape), op0=ALU.mult, op1=ALU.mult,
                )
                res.append(prod)
            return res

        def a_finish(t, j, res, adder):
            adder.tensor_tensor(out=res[1][:], in0=res[1][:], in1=res[0][:], op=ALU.subtract)

        def a_store(t, j, res):
            nc.sync.dma_start(out=outs[1][t * P : (t + 1) * P, j * 512 : (j + 1) * 512], in_=res[1][:])

        def mx_job(gi, job):
            proj, t0, nt = GROUPS[gi][:3]
            cs = slice(t0 % 4 * P, (t0 % 4 + nt) * P)
            acc = psum.tile([P, QUAD // nt, nt * P], F32, name="acc", tag="acc", bufs=MX_BANKS)
            for i, h in enumerate(job_heads(gi, job)):
                wt, hl = wcodes[proj, h]
                for g in range(PASSES):
                    nc.tensor.matmul_mx(
                        out=acc[:, i, :],
                        lhsT=wt[:, g, hl * 2 * HD : (hl + 1) * 2 * HD].bitcast(FP4X4),
                        lhsT_scale=planes[proj][:, g, h * HD : (h + 1) * HD],
                        rhs=xcodes[t0 // 4, g][:, cs].bitcast(FP8X4),
                        rhs_scale=xscales[t0 // 4, g][:, cs],
                        start=(g == 0),
                        stop=(g == PASSES - 1),
                    )
            return acc

        def drain_job(gi, job, acc, sq):
            proj, t0, nt = GROUPS[gi][:3]
            w = work.tile([P, QUAD * P], F32, name="w", tag="w", bufs=W_BUFS)
            n = nt * P
            for i, h in enumerate(job_heads(gi, job)):
                nc.scalar.activation(
                    out=w[:, i * n : (i + 1) * n], in_=acc[:, i, :], func=ACT.Identity,
                    scale=cols[proj][:, NH + h : NH + h + 1], bias=gb[proj][:, h : h + 1],
                )
            for i, h in enumerate(job_heads(gi, job)):
                nc.scalar.activation(
                    out=sq[:, i * n : (i + 1) * n], in_=acc[:, i, :], func=ACT.Square, bias=cols[proj][:, h : h + 1]
                )
            return w

        def rotate_job(gi, job, w):
            proj, t0, nt = GROUPS[gi][:3]
            hb, n = QUAD // nt, nt * P
            for name in ("cosT", "sinT"):
                tab = state[name, t0 // 4][:, t0 % 4 : t0 % 4 + nt, :].rearrange("p (o t) l -> p o (t l)", o=1)
                prod = work.tile([P, hb, n], F32, name="prod", tag="prod", bufs=PROD_BUFS)
                nc.vector.tensor_tensor(
                    out=prod[:], in0=w[:].rearrange("p (h l) -> p h l", h=hb), in1=tab.to_broadcast([P, hb, n]), op=ALU.mult
                )
                for i, h in enumerate(job_heads(gi, job)):
                    state[name, gi, h] = prod[:, i, :]

        def ss_transpose(gi, parts):
            nt = GROUPS[gi][2]
            bank = psum.tile([P, nt, P], F32, name="ss", tag="tbank", bufs=T_BANKS)
            for t in range(nt):
                blocks = [sq[:, b * P : (b + 1) * P] for sq in parts for b in range(t, sq.shape[1] // P, nt)]
                for i, blk in enumerate(blocks):
                    nc.tensor.matmul(
                        out=bank[:, t, :], lhsT=blk, rhs=ident[:],
                        start=(i == 0), stop=(i == len(blocks) - 1), is_transpose=True,
                    )
            state["ss", gi] = bank

        def ss_reduce(gi):
            nt = GROUPS[gi][2]
            total = work.tile([P, nt], F32, name="total", tag="total", bufs=2)
            nc.vector.tensor_reduce(out=total[:], in_=state["ss", gi][:], axis=AXIS.X, op=ALU.add)
            state["total", gi] = total

        def ss_rstd(key, nt):
            var = work.tile([P, nt], F32, name="var", tag="var", bufs=2)
            nc.gpsimd.tensor_scalar(
                out=var[:], in0=state[("total",) + key][:], scalar1=1.0 / D, scalar2=EPS, op0=ALU.mult, op1=ALU.add
            )
            rstd = work.tile([P, nt], F32, name="rstd", tag="rstd", bufs=4)
            nc.gpsimd.tensor_tensor(out=rstd[:], in0=var[:], in1=minus_half[:, 0:nt], op=ALU.pow)
            state[("rstd",) + key] = rstd

        def unit_transpose(gi, t, hq, spare=False):
            if spare:
                bank = psum.tile([P, QUAD, HD], F32, name="obank", tag="acc", bufs=MX_BANKS)
            else:
                bank = psum.tile([P, QUAD, HD], F32, name="obank", tag="tbank", bufs=T_BANKS)
            for i in range(QUAD):
                h = hq * QUAD + i
                ts = slice(t * P, (t + 1) * P)
                nc.tensor.matmul(
                    out=bank[:, i, :], lhsT=state["cosT", gi, h][:, ts], rhs=ident[:], start=True, stop=False, is_transpose=True
                )
                nc.tensor.matmul(
                    out=bank[:, i, :], lhsT=state["sinT", gi, h][:, ts], rhs=swap[:], start=False, stop=True, is_transpose=True
                )
            return bank

        def unit_finish(gi, t, hq, bank, on_vector):
            proj, t0, nt = GROUPS[gi][:3]
            y = work.tile([P, QUAD * HD], F32, name="y", tag="y", bufs=Y_BUFS)
            r = state["rstd", gi][:, t : t + 1]
            src = bank[:].rearrange("p h d -> p (h d)")
            if on_vector:
                nc.vector.tensor_scalar(out=y[:], in0=src, scalar1=r, scalar2=None, op0=ALU.mult)
            else:
                nc.scalar.activation(out=y[:], in_=src, func=ACT.Copy, scale=r)
            nc.sync.dma_start(
                out=outs[proj][(t0 + t) * P : (t0 + t + 1) * P, hq * QUAD * HD : (hq + 1) * QUAD * HD], in_=y[:]
            )

        steps = []
        for gi in range(len(GROUPS)):
            jobs = NH * GROUPS[gi][2] // QUAD
            steps.extend((gi, list(range(j, min(j + STEP, jobs)))) for j in range(0, jobs, STEP))
        a_units = [(t, j) for t in range(A_TILES) for j in range(3)]
        early = a_units[: 3 * A_EARLY]
        a_at = {A_START + (i * A_SPAN) // len(early): u for i, u in enumerate(early)}
        a_at.update({len(steps) + A_LATE_AT + i: u for i, u in enumerate(a_units[3 * A_EARLY :])})
        last_mx = max(list(a_at) + [len(steps) - 1])
        a_prod_at = {}
        a_stores = []
        units = []
        closing = {}
        parts = {}
        prev_w = []
        count = 0
        si = 0
        while si <= last_mx or units or any(s >= si for s in closing) or prev_w or any(s + A_STORE_DELAY >= si for s in a_prod_at):
            live = si < len(steps)
            accs = []
            a_now = a_at.get(si)
            if a_now is not None:
                a_acc = a_matmul(*a_now)
            if live:
                gi, jobs = steps[si]
                for job in jobs:
                    accs.append((job, mx_job(gi, job)))
            if si == 0:
                tables()
            if si == A_START and A_TILES:
                table_tokens()
            if si == K_PARAMS - 1:
                widen_rows(1)
            if si == K_PARAMS:
                params(1)
            if prev_w and ("cosT", GROUPS[prev_w[0][0]][1] // 4) not in state:
                table_transpose(GROUPS[prev_w[0][0]][1] // 4)
            xs = []
            if live and later and si >= X_START:
                for it in later[:X_PER_STEP]:
                    xs.append((it, x_transpose(*it)))
                later = later[X_PER_STEP:]
            cgi = closing.get(si)
            ready = [u for u in units if u[3] <= si]
            take = min(UNITS_PER_STEP + (si >= CATCH_UP) if si <= last_mx else TAIL_TAKE, (T_BANKS if si <= last_mx + 1 else 4) - len(xs) - (cgi is not None))
            now = ready[:take]
            units = [u for u in units if u not in now]
            banks = [unit_transpose(*u[:3], spare=(si > last_mx + 1 and i % 2 == 1)) for i, u in enumerate(now)]
            if cgi is not None:
                ss_transpose(cgi, parts[cgi])
            if a_now is not None:
                a_bias(a_now[0], a_now[1], a_acc)
            for pgi, job, w in prev_w:
                rotate_job(pgi, job, w)
            prev_w = []
            a_res = [(u, a_products(*u)) for u in a_prod_at.get(si, [])]
            if live:
                sq = work.tile([P, len(accs) * QUAD * P], F32, name="sq", tag="sq", bufs=SQ_BUFS)
            for i, (job, acc) in enumerate(accs):
                w = drain_job(gi, job, acc, sq[:, i * QUAD * P : (i + 1) * QUAD * P])
                prev_w.append((gi, job, w))
            if a_now is not None:
                a_square(*a_now)
                if 3 * a_now[0] + a_now[1] >= 3 * A_TILES - A_V_GAINS:
                    a_gain(a_now[0], a_now[1], nc.vector)
                elif a_now[1] < 2:
                    a_gain(a_now[0], a_now[1], nc.gpsimd)
            for u, res in a_res:
                a_finish(u[0], u[1], res, nc.vector if 3 * u[0] + u[1] >= 3 * A_TILES - A_V_ADDS else nc.gpsimd)
            a_stores.extend((si + A_STORE_DELAY, u, res) for u, res in a_res)
            for i, (it, bank) in enumerate(xs):
                x_copy(it[0], it[1], it[2], bank, on_scalar=i < X_ON_SCALAR)
            for u, bank in zip(now, banks):
                count += 1
                unit_finish(u[0], u[1], u[2], bank, on_vector=(count % V_EVERY < V_NUM) if live else (count % TAIL_V == 0 and si > last_mx + 3))
            for due, u, res in a_stores:
                if due == si:
                    a_store(u[0], u[1], res)
            if cgi is not None:
                ss_reduce(cgi)
                units.extend(
                    (cgi, t, hq, si + UNIT_DELAY) for hq in range(NH // QUAD) for t in range(GROUPS[cgi][2])
                )
            if a_now is not None and a_now[1] == 2:
                a_total(a_now[0])
                for j in range(3):
                    a_prod_at.setdefault(si + (A_DELAY + (j * A_SPAN) // len(early) if a_now[0] < A_EARLY else 1 + j), []).append((a_now[0], j))
            for it, bank in xs:
                if it[2] + 2 >= CHUNKS[it[0]][1]:
                    x_quantize(it[0], it[1])
            if live:
                nt, unfolded = GROUPS[gi][2:4]
                njobs = NH * nt // QUAD
                if jobs[0] == 0:
                    parts[gi] = [sq]
                elif jobs[0] < njobs - unfolded * STEP:
                    acc_sq = work.tile([P, STEP * QUAD * P], F32, name="sqsum", tag="sqsum", bufs=2)
                    nc.gpsimd.tensor_tensor(out=acc_sq[:], in0=parts[gi][0][:], in1=sq[:], op=ALU.add)
                    parts[gi][0] = acc_sq
                else:
                    parts[gi].append(sq)
                if jobs[-1] == njobs - 1:
                    assert si + GROUPS[gi][4] not in closing
                    closing[si + GROUPS[gi][4]] = gi
            if cgi is not None:
                ss_rstd((cgi,), GROUPS[cgi][2])
            if a_now is not None and a_now[1] == 2:
                ss_rstd(("a", a_now[0]), 1)
                if 3 * a_now[0] + a_now[1] < 3 * A_TILES - A_V_GAINS:
                    a_gain(a_now[0], a_now[1], nc.gpsimd)
            si += 1
